import numpy as np
import ml_dtypes


def mxq(x, axis, fmt="e4m3"):
    dtype, down = {"e4m3": (ml_dtypes.float8_e4m3fn, 7), "e5m2": (ml_dtypes.float8_e5m2, 14)}[fmt]
    v = np.moveaxis(np.asarray(x, np.float32).astype(ml_dtypes.bfloat16).astype(np.float64), axis, -1)
    blocks = v.reshape(v.shape[:-1] + (-1, 32))
    amax = np.abs(blocks).max(-1, keepdims=True)
    byte = np.maximum(np.where(amax > 0, np.frexp(amax)[1] - 1 + 127, 0) - down, 1)
    scale = np.exp2(byte - 127.0)
    codes = (blocks / scale).astype(np.float32).astype(dtype).astype(np.float64)
    return np.moveaxis((codes * scale).reshape(v.shape), -1, axis)


WIDE = False


def mx_kscale(k):
    if not WIDE:
        return np.ones(k)
    levels = np.array([10, -10, 5, -5, 0])
    if k % 512:
        return np.exp2(np.random.permutation(np.resize(levels, k // 32))).repeat(32)
    a = np.empty((k // 512, 16))
    for p in range(k // 512):
        a[p, :8] = np.random.permutation(np.resize(levels, 8))
        for g in range(8):
            far = levels[np.abs(levels - a[p, g]) >= 10]
            a[p, g + 8] = far[np.random.randint(len(far))]
    return np.exp2(a.ravel()).repeat(32)


BF16 = ml_dtypes.bfloat16


def bf(x):
    return np.asarray(x, np.float32).astype(BF16)


def f64(x):
    return np.asarray(x).astype(np.float64)


B, T, N, D, L = 1, 8, 128, 1024, 512


def setup_inputs():
    s, r = mx_kscale(D), mx_kscale(L)
    x = np.random.standard_normal((B, T, N, D)) + 0.5 * np.random.standard_normal(D)
    return {"x": bf(x * s),
            "Wtheta": bf(np.random.standard_normal((L, D)) / np.sqrt(D) / s * r[:, None]),
            "Wphi": bf(np.random.standard_normal((L, D)) / np.sqrt(D) / s / r[:, None])}


def reference(x, Wtheta, Wphi):
    xq = mxq(f64(x), 3, "e4m3")
    th = xq @ mxq(f64(Wtheta), 1, "e4m3").T
    ph = xq @ mxq(f64(Wphi), 1, "e4m3").T
    thq, phq = mxq(th, 3, "e4m3"), mxq(ph, 3, "e4m3")
    sw = (thq @ phq.transpose(0, 1, 3, 2)) / N
    tw = (thq.transpose(0, 2, 1, 3) @ phq.transpose(0, 2, 3, 1)).transpose(0, 2, 1, 3) / T
    return sw, tw

@@ -1,0 +1,234 @@
+from contextlib import ExitStack
+
+import concourse.mybir as mybir
+from concourse.masks import make_identity
+
+F32 = mybir.dt.float32
+BF16 = mybir.dt.bfloat16
+U32 = mybir.dt.uint32
+I32 = mybir.dt.int32
+U8 = mybir.dt.uint8
+FP8X4 = mybir.dt.float8_e4m3fn_x4
+ALU = mybir.AluOpType
+AX = mybir.AxisListType
+
+P = 128
+FRAMES = 8
+FEATURES = 1024
+LATENT = 512
+PACK = 4
+PASSES = FEATURES // (P * PACK)
+BANK = 512
+GROUP = 16
+GROUPS = P // GROUP
+THETA = 0
+PHI = 1
+FLOPS = 2 * (FRAMES * P) * FEATURES * (2 * LATENT) + 2 * FRAMES * P * P * LATENT + 2 * P * FRAMES * FRAMES * LATENT
+
+VECTOR_EMPTIES = (("phi", 0), ("phi", 3), ("x", 4), ("x", 7))
+WARM_BEFORE = 5
+
+
+def tile_higcin_volleyball_pa_kernel(tc, x, Wtheta, Wphi, out_0, out_1):
+    nc = tc.nc
+    with ExitStack() as ctx:
+        ctx.enter_context(tc.manual_schedule())
+        raw = ctx.enter_context(tc.tile_pool(name="raw", bufs=1))
+        keep = ctx.enter_context(tc.tile_pool(name="keep", bufs=1))
+        stage = ctx.enter_context(tc.tile_pool(name="stage", bufs=6))
+        flip_banks = ctx.enter_context(tc.psum_pool(name="flip", bufs=3))
+        proj_banks = ctx.enter_context(tc.psum_pool(name="proj", bufs=4))
+        first_bank = ctx.enter_context(tc.psum_pool(name="first", bufs=1))
+
+        theta_tiles = [("theta", i) for i in range(PACK)]
+        phi_tiles = [("phi", i) for i in range(PACK)]
+        x_tiles = [("x", f) for f in range(FRAMES)]
+
+        dram = {}
+        for i in range(PACK):
+            dram[("theta", i)] = Wtheta.rearrange("(p i) d -> p i d", i=PACK)[:, i, :]
+            dram[("phi", i)] = Wphi.rearrange("(p i) d -> p i d", i=PACK)[:, i, :]
+        for f in range(FRAMES):
+            dram[("x", f)] = x[0, f]
+        rows = {}
+        codes = {}
+        scales = {}
+        for key in theta_tiles + x_tiles[0:3] + phi_tiles + x_tiles[3:8]:
+            label = "%s%d" % key
+            rows[key] = raw.tile([P, FEATURES], BF16, name="rows_" + label)
+            codes[key] = keep.tile([P, PASSES * P], U32, name="codes_" + label, align_bytes=64)
+            scales[key] = keep.tile([P, PASSES * P], U8, name="scales_" + label, align_bytes=64)
+            nc.sync.dma_start(out=rows[key][:], in_=dram[key])
+
+        zeros = keep.tile([P, BANK], BF16, name="zeros")
+        nc.vector.memset(zeros[:], 0.0)
+        table_load = keep.tile([P, 1], F32, name="table_load")
+        nc.scalar.mul(out=table_load[:], in_=zeros[:, 0:1], mul=1.0)
+        ident = keep.tile([P, P], F32, name="ident")
+        make_identity(nc, ident[:])
+        h_codes = [keep.tile([P, 2 * P], U32, name="h_codes%d" % f, align_bytes=64) for f in range(FRAMES)]
+        h_scales = [keep.tile([P, 2 * P], U8, name="h_scales%d" % f, align_bytes=64) for f in range(FRAMES)]
+        for f in range(FRAMES):
+            nc.vector.memset(h_scales[f][:].bitcast(I32), 0)
+        block_sum = keep.tile([P, GROUP], F32, name="block_sum")
+        nc.vector.tensor_reduce(
+            out=block_sum[:], in_=ident[:].rearrange("p (t j) -> p j t", j=GROUP), axis=AX.X, op=ALU.add
+        )
+        same_node = keep.tile([P, GROUP], F32, name="same_node")
+        nc.vector.tensor_scalar_mul(out=same_node[:], in0=block_sum[:], scalar1=1.0 / FRAMES)
+        g_codes = keep.tile([P, GROUPS * 2 * P], U32, name="g_codes", align_bytes=64)
+        g_scales = keep.tile([P, GROUPS * 2 * P], U8, name="g_scales", align_bytes=64)
+        g_codes_view = g_codes[:].bitcast(I32).rearrange("p (g w t j) -> p g w t j", g=GROUPS, w=2, t=FRAMES)
+        g_scales_view = g_scales[:].bitcast(I32).rearrange("p (g w t j) -> p g w t j", g=GROUPS, w=2, t=FRAMES)
+        masked = keep.tile([P, GROUPS * FRAMES, GROUP], F32, name="masked")
+        tw_rows = keep.tile([P, GROUPS * FRAMES], F32, name="tw_rows")
+        warm_bank = first_bank.tile([P, BANK], F32, tag="first", name="warm_bank")
+
+        def warm_up():
+            nc.tensor.matmul(out=warm_bank[:], lhsT=zeros[:, 0:P], rhs=zeros[:], start=True, stop=True)
+
+        def transpose_run(keys, warm=False):
+            copied = []
+            for key in keys:
+                bank = flip_banks.tile([P, PASSES, 2, P], F32, tag="flip", name="bank")
+                words = rows[key][:].bitcast(F32)
+                for c in range(PASSES):
+                    for h in range(2):
+                        every_2nd = slice(2 * c * P + h, 2 * (c + 1) * P, 2)
+                        nc.tensor.transpose(bank[:, c, h, :], words[:, every_2nd], ident[:])
+                if warm:
+                    warm_up()
+                grouped = stage.tile([P, FEATURES], BF16, tag="grouped", name="grouped", align_bytes=64)
+                target = grouped[:].bitcast(F32).rearrange("p (c r h) -> p c r h", c=PASSES, h=2)
+                source = bank[:].rearrange("p c h r -> p c r h")
+                if key in VECTOR_EMPTIES:
+                    nc.vector.tensor_copy(out=target, in_=source)
+                else:
+                    nc.scalar.copy(out=target, in_=source)
+                copied.append((key, grouped))
+                if len(copied) > 1:
+                    quantise_tile(*copied[-2])
+            quantise_tile(*copied[-1])
+
+        def quantise_tile(key, grouped):
+            nc.vector.quantize_mx(out=codes[key][:].bitcast(FP8X4), scales=scales[key][:], in_=grouped[:])
+
+        h_grouped = {}
+        unmoved = {}
+
+        def project_run(pairs):
+            for f, w in pairs:
+                bank = proj_banks.tile([P, PACK, P], F32, tag="proj", name="bank")
+                for i in range(PACK):
+                    weight = (("theta", i), ("phi", i))[w]
+                    for c in range(PASSES):
+                        cols = slice(c * P, (c + 1) * P)
+                        nc.tensor.matmul_mx(
+                            out=bank[:, i, :],
+                            lhsT=codes[weight][:, cols].bitcast(FP8X4),
+                            lhsT_scale=scales[weight][:, cols],
+                            rhs=codes[("x", f)][:, cols].bitcast(FP8X4),
+                            rhs_scale=scales[("x", f)][:, cols],
+                            start=(c == 0),
+                            stop=(c == PASSES - 1),
+                        )
+                if f not in h_grouped:
+                    h_grouped[f] = stage.tile([P, 2, P, PACK], BF16, tag="h_grouped", name="h_grouped", align_bytes=64)
+                nc.scalar.copy(out=h_grouped[f][:, w, :, :], in_=bank[:].rearrange("p i r -> p r i"))
+                if f == FRAMES - 1:
+                    quantise_h(f, w, w + 1)
+                elif w == PHI:
+                    quantise_h(f, THETA, PHI + 1)
+
+        def quantise_h(f, w_from, w_to):
+            cols = slice(w_from * P, w_to * P)
+            nc.vector.quantize_mx(
+                out=h_codes[f][:, cols].bitcast(FP8X4),
+                scales=h_scales[f][:, cols],
+                in_=h_grouped[f][:, w_from:w_to, :, :].rearrange("p w r i -> p (w r i)"),
+            )
+            move_unmoved()
+            unmoved["piece"] = (f, w_from, w_to)
+
+        def move_unmoved():
+            if "piece" not in unmoved:
+                return
+            f, w_from, w_to = unmoved["piece"]
+            for plain, by_group, run in ((h_codes, g_codes_view, GROUP), (h_scales, g_scales_view, GROUP // 4)):
+                nc.vector.tensor_copy(
+                    out=by_group[:, :, w_from:w_to, f, :],
+                    in_=plain[f][:]
+                    .bitcast(I32)[:, w_from * GROUPS * run : w_to * GROUPS * run]
+                    .rearrange("p (w g j) -> p g w j", g=GROUPS, j=run),
+                )
+
+        def spatial(bank, f):
+            nc.tensor.matmul_mx(
+                out=bank[:, f % 4, :],
+                lhsT=h_codes[f][:, 0:P].bitcast(FP8X4),
+                lhsT_scale=h_scales[f][:, 0:P],
+                rhs=h_codes[f][:, P : 2 * P].bitcast(FP8X4),
+                rhs_scale=h_scales[f][:, P : 2 * P],
+                start=True,
+                stop=True,
+            )
+
+        def store_spatial(bank, f_from):
+            sw_rows = stage.tile([P, 4, P], F32, tag="sw_rows", name="sw_rows")
+            nc.scalar.mul(out=sw_rows[:], in_=bank[:], mul=1.0 / P)
+            nc.sync.dma_start(out=out_0[0, f_from : f_from + 4].rearrange("t j k -> j t k"), in_=sw_rows[:])
+
+        def temporal(half):
+            bank = flip_banks.tile([P, 4, P], F32, tag="flip", name="bank")
+            for i in range(4):
+                first = (4 * half + i) * 2 * P
+                nc.tensor.matmul_mx(
+                    out=bank[:, i, :],
+                    lhsT=g_codes[:, first : first + P].bitcast(FP8X4),
+                    lhsT_scale=g_scales[:, first : first + P],
+                    rhs=g_codes[:, first + P : first + 2 * P].bitcast(FP8X4),
+                    rhs_scale=g_scales[:, first + P : first + 2 * P],
+                    start=True,
+                    stop=True,
+                )
+            return bank
+
+        def keep_same_node(bank, half):
+            nc.vector.tensor_tensor(
+                out=masked[:, 32 * half : 32 * half + 32, :],
+                in0=bank[:].rearrange("p g (s j) -> p (g s) j", j=GROUP),
+                in1=same_node[:].unsqueeze(1).to_broadcast([P, 32, GROUP]),
+                op=ALU.mult,
+            )
+
+        for i in range(WARM_BEFORE):
+            warm_up()
+        transpose_run(theta_tiles + x_tiles[0:3], warm=True)
+        project_run([(0, THETA), (1, THETA)])
+        transpose_run(phi_tiles)
+        project_run([(2, THETA)])
+        transpose_run(x_tiles[3:6])
+        project_run([(0, PHI), (1, PHI), (2, PHI), (3, THETA), (3, PHI)])
+        transpose_run(x_tiles[6:8])
+        project_run([(f, w) for f in range(4, FRAMES) for w in (THETA, PHI)])
+        move_unmoved()
+
+        sw_early = first_bank.tile([P, 4, P], F32, tag="first", name="sw_early")
+        sw_late = proj_banks.tile([P, 4, P], F32, tag="proj", name="sw_late")
+        for f in range(4):
+            spatial(sw_early, f)
+        store_spatial(sw_early, 0)
+        for f in range(4, FRAMES - 1):
+            spatial(sw_late, f)
+        tw_banks = [temporal(0), temporal(1)]
+        spatial(sw_late, FRAMES - 1)
+        keep_same_node(tw_banks[0], 0)
+        store_spatial(sw_late, 4)
+        keep_same_node(tw_banks[1], 1)
+        nc.vector.tensor_reduce(out=tw_rows[:], in_=masked[:], axis=AX.X, op=ALU.add)
+        for t in range(FRAMES):
+            queue = nc.sync if t % 2 == 0 else nc.scalar
+            queue.dma_start(
+                out=out_1[0, t].rearrange("(g j) s -> j g s", j=GROUP),
+                in_=tw_rows[GROUP * t : GROUP * (t + 1), :].rearrange("p (g s) -> p g s", s=FRAMES),
+            )

@@ -78,8 +78,8 @@ def tile_higcin_volleyball_pa_kernel(tc, x, Wtheta, Wphi, out_0, out_1):
         nc.vector.tensor_scalar_mul(out=same_node[:], in0=block_sum[:], scalar1=1.0 / FRAMES)
         g_codes = keep.tile([P, GROUPS * 2 * P], U32, name="g_codes", align_bytes=64)
         g_scales = keep.tile([P, GROUPS * 2 * P], U8, name="g_scales", align_bytes=64)
-        g_codes_view = g_codes[:].bitcast(I32).rearrange("p (g w t j) -> p g w t j", g=GROUPS, w=2, t=FRAMES)
-        g_scales_view = g_scales[:].bitcast(I32).rearrange("p (g w t j) -> p g w t j", g=GROUPS, w=2, t=FRAMES)
+        g_codes_view = g_codes[:].bitcast(I32).rearrange("p (g w t j) -> p w g t j", g=GROUPS, w=2, t=FRAMES)
+        g_scales_view = g_scales[:].rearrange("p (g w t j) -> p w g t j", g=GROUPS, w=2, t=FRAMES)
         masked = keep.tile([P, GROUPS * FRAMES, GROUP], F32, name="masked")
         tw_rows = keep.tile([P, GROUPS * FRAMES], F32, name="tw_rows")
         warm_bank = first_bank.tile([P, BANK], F32, tag="first", name="warm_bank")
@@ -154,12 +154,11 @@ def tile_higcin_volleyball_pa_kernel(tc, x, Wtheta, Wphi, out_0, out_1):
             if "piece" not in unmoved:
                 return
             f, w_from, w_to = unmoved["piece"]
-            for plain, by_group, run in ((h_codes, g_codes_view, GROUP), (h_scales, g_scales_view, GROUP // 4)):
+            cols = slice(w_from * P, w_to * P)
+            for plain, by_group in ((h_codes[f][:].bitcast(I32), g_codes_view), (h_scales[f][:], g_scales_view)):
                 nc.vector.tensor_copy(
-                    out=by_group[:, :, w_from:w_to, f, :],
-                    in_=plain[f][:]
-                    .bitcast(I32)[:, w_from * GROUPS * run : w_to * GROUPS * run]
-                    .rearrange("p (w g j) -> p g w j", g=GROUPS, j=run),
+                    out=by_group[:, w_from:w_to, :, f, :],
+                    in_=plain[:, cols].rearrange("p (w j g) -> p w g j", j=GROUP, g=GROUPS),
                 )
 
         def spatial(bank, f):
@@ -173,10 +172,11 @@ def tile_higcin_volleyball_pa_kernel(tc, x, Wtheta, Wphi, out_0, out_1):
                 stop=True,
             )
 
-        def store_spatial(bank, f_from):
+        def store_spatial(bank, f_from, f_to):
             sw_rows = stage.tile([P, 4, P], F32, tag="sw_rows", name="sw_rows")
-            nc.scalar.mul(out=sw_rows[:], in_=bank[:], mul=1.0 / P)
-            nc.sync.dma_start(out=out_0[0, f_from : f_from + 4].rearrange("t j k -> j t k"), in_=sw_rows[:])
+            used = slice(f_from % 4, (f_to - 1) % 4 + 1)
+            nc.scalar.mul(out=sw_rows[:, used, :], in_=bank[:, used, :], mul=1.0 / P)
+            nc.sync.dma_start(out=out_0[0, f_from:f_to].rearrange("t j k -> j t k"), in_=sw_rows[:, used, :])
 
         def temporal(half):
             bank = flip_banks.tile([P, 4, P], F32, tag="flip", name="bank")
@@ -215,20 +215,22 @@ def tile_higcin_volleyball_pa_kernel(tc, x, Wtheta, Wphi, out_0, out_1):
 
         sw_early = first_bank.tile([P, 4, P], F32, tag="first", name="sw_early")
         sw_late = proj_banks.tile([P, 4, P], F32, tag="proj", name="sw_late")
+        sw_last = proj_banks.tile([P, 4, P], F32, tag="proj", name="sw_last")
         for f in range(4):
             spatial(sw_early, f)
-        store_spatial(sw_early, 0)
+        store_spatial(sw_early, 0, 4)
         for f in range(4, FRAMES - 1):
             spatial(sw_late, f)
+        store_spatial(sw_late, 4, FRAMES - 1)
+        spatial(sw_last, FRAMES - 1)
+        store_spatial(sw_last, FRAMES - 1, FRAMES)
         tw_banks = [temporal(0), temporal(1)]
-        spatial(sw_late, FRAMES - 1)
         keep_same_node(tw_banks[0], 0)
-        store_spatial(sw_late, 4)
         keep_same_node(tw_banks[1], 1)
-        nc.vector.tensor_reduce(out=tw_rows[:], in_=masked[:], axis=AX.X, op=ALU.add)
-        for t in range(FRAMES):
-            queue = nc.sync if t % 2 == 0 else nc.scalar
-            queue.dma_start(
-                out=out_1[0, t].rearrange("(g j) s -> j g s", j=GROUP),
-                in_=tw_rows[GROUP * t : GROUP * (t + 1), :].rearrange("p (g s) -> p g s", s=FRAMES),
+        for half in range(2):
+            pairs = slice(32 * half, 32 * half + 32)
+            nc.vector.tensor_reduce(out=tw_rows[:, pairs], in_=masked[:, pairs, :], axis=AX.X, op=ALU.add)
+            nc.sync.dma_start(
+                out=out_1[0].rearrange("t n s -> (t n) s").rearrange("(p g) s -> p (g s)", g=GROUPS)[:, pairs],
+                in_=tw_rows[:, pairs],
             )

@@ -25,7 +25,9 @@ THETA = 0
 PHI = 1
 FLOPS = 2 * (FRAMES * P) * FEATURES * (2 * LATENT) + 2 * FRAMES * P * P * LATENT + 2 * P * FRAMES * FRAMES * LATENT
 
-VECTOR_EMPTIES = (("phi", 0), ("phi", 3), ("x", 4), ("x", 7))
+VECTOR_EMPTIES = (("x", 5), ("x", 6))
+UNSORTED = 6
+SORT_AHEAD = 3
 WARM_BEFORE = 5
 
 
@@ -43,6 +45,7 @@ def tile_higcin_volleyball_pa_kernel(tc, x, Wtheta, Wphi, out_0, out_1):
         theta_tiles = [("theta", i) for i in range(PACK)]
         phi_tiles = [("phi", i) for i in range(PACK)]
         x_tiles = [("x", f) for f in range(FRAMES)]
+        tiles = theta_tiles + x_tiles[0:3] + phi_tiles + x_tiles[3:8]
 
         dram = {}
         for i in range(PACK):
@@ -53,7 +56,7 @@ def tile_higcin_volleyball_pa_kernel(tc, x, Wtheta, Wphi, out_0, out_1):
         rows = {}
         codes = {}
         scales = {}
-        for key in theta_tiles + x_tiles[0:3] + phi_tiles + x_tiles[3:8]:
+        for key in tiles:
             label = "%s%d" % key
             rows[key] = raw.tile([P, FEATURES], BF16, name="rows_" + label)
             codes[key] = keep.tile([P, PASSES * P], U32, name="codes_" + label, align_bytes=64)
@@ -87,28 +90,45 @@ def tile_higcin_volleyball_pa_kernel(tc, x, Wtheta, Wphi, out_0, out_1):
         def warm_up():
             nc.tensor.matmul(out=warm_bank[:], lhsT=zeros[:, 0:P], rhs=zeros[:], start=True, stop=True)
 
+        ordered = {}
+        waiting = []
+
+        def quantise_waiting(keep_back):
+            while len(waiting) > keep_back:
+                step = waiting.pop(0)
+                step[0](*step[1:])
+
+        def sort_words(key):
+            ordered[key] = stage.tile([P, PASSES, 2, P], F32, tag="ordered", name="ordered")
+            nc.vector.tensor_copy(
+                out=ordered[key][:], in_=rows[key][:].bitcast(F32).rearrange("p (c r h) -> p c h r", c=PASSES, h=2)
+            )
+
         def transpose_run(keys, warm=False):
-            copied = []
             for key in keys:
+                place = tiles.index(key)
+                for ahead in tiles[max(place, UNSORTED) : place + SORT_AHEAD + 1]:
+                    if ahead not in ordered:
+                        sort_words(ahead)
                 bank = flip_banks.tile([P, PASSES, 2, P], F32, tag="flip", name="bank")
-                words = rows[key][:].bitcast(F32)
+                words = rows[key][:].bitcast(F32).rearrange("p (c r h) -> p c h r", c=PASSES, h=2)
+                if key in ordered:
+                    words = ordered[key][:]
                 for c in range(PASSES):
                     for h in range(2):
-                        every_2nd = slice(2 * c * P + h, 2 * (c + 1) * P, 2)
-                        nc.tensor.transpose(bank[:, c, h, :], words[:, every_2nd], ident[:])
+                        nc.tensor.transpose(bank[:, c, h, :], words[:, c, h, :], ident[:])
                 if warm:
                     warm_up()
                 grouped = stage.tile([P, FEATURES], BF16, tag="grouped", name="grouped", align_bytes=64)
                 target = grouped[:].bitcast(F32).rearrange("p (c r h) -> p c r h", c=PASSES, h=2)
                 source = bank[:].rearrange("p c h r -> p c r h")
                 if key in VECTOR_EMPTIES:
+                    quantise_waiting(0)
                     nc.vector.tensor_copy(out=target, in_=source)
                 else:
                     nc.scalar.copy(out=target, in_=source)
-                copied.append((key, grouped))
-                if len(copied) > 1:
-                    quantise_tile(*copied[-2])
-            quantise_tile(*copied[-1])
+                waiting.append((quantise_tile, key, grouped))
+                quantise_waiting(1)
 
         def quantise_tile(key, grouped):
             nc.vector.quantize_mx(out=codes[key][:].bitcast(FP8X4), scales=scales[key][:], in_=grouped[:])
@@ -136,9 +156,10 @@ def tile_higcin_volleyball_pa_kernel(tc, x, Wtheta, Wphi, out_0, out_1):
                     h_grouped[f] = stage.tile([P, 2, P, PACK], BF16, tag="h_grouped", name="h_grouped", align_bytes=64)
                 nc.scalar.copy(out=h_grouped[f][:, w, :, :], in_=bank[:].rearrange("p i r -> p r i"))
                 if f == FRAMES - 1:
-                    quantise_h(f, w, w + 1)
+                    waiting.append((quantise_h, f, w, w + 1))
                 elif w == PHI:
-                    quantise_h(f, THETA, PHI + 1)
+                    waiting.append((quantise_h, f, THETA, PHI + 1))
+                quantise_waiting(1)
 
         def quantise_h(f, w_from, w_to):
             cols = slice(w_from * P, w_to * P)
@@ -203,14 +224,20 @@ def tile_higcin_volleyball_pa_kernel(tc, x, Wtheta, Wphi, out_0, out_1):
 
         for i in range(WARM_BEFORE):
             warm_up()
-        transpose_run(theta_tiles + x_tiles[0:3], warm=True)
-        project_run([(0, THETA), (1, THETA)])
-        transpose_run(phi_tiles)
+        transpose_run(theta_tiles)
+        transpose_run(x_tiles[0:3], warm=True)
+        transpose_run(phi_tiles[0:1])
+        project_run([(0, THETA)])
+        transpose_run(phi_tiles[1:3])
+        project_run([(1, THETA)])
+        transpose_run(phi_tiles[3:4] + x_tiles[3:4])
         project_run([(2, THETA)])
-        transpose_run(x_tiles[3:6])
-        project_run([(0, PHI), (1, PHI), (2, PHI), (3, THETA), (3, PHI)])
+        transpose_run(x_tiles[4:6])
+        project_run([(0, PHI), (3, THETA), (1, PHI)])
         transpose_run(x_tiles[6:8])
-        project_run([(f, w) for f in range(4, FRAMES) for w in (THETA, PHI)])
+        project_run([(2, PHI), (4, THETA), (3, PHI), (4, PHI)])
+        project_run([(f, w) for f in range(5, FRAMES) for w in (THETA, PHI)])
+        quantise_waiting(0)
         move_unmoved()
 
         sw_early = first_bank.tile([P, 4, P], F32, tag="first", name="sw_early")

@@ -21,6 +21,9 @@ PASSES = FEATURES // (P * PACK)
 BANK = 512
 GROUP = 16
 GROUPS = P // GROUP
+HALVES = 2
+HALF = GROUP // HALVES
+CHUNK = FRAMES * HALF
 THETA = 0
 PHI = 1
 FLOPS = 2 * (FRAMES * P) * FEATURES * (2 * LATENT) + 2 * FRAMES * P * P * LATENT + 2 * P * FRAMES * FRAMES * LATENT
@@ -29,6 +32,7 @@ VECTOR_EMPTIES = (("x", 5), ("x", 6))
 UNSORTED = 6
 SORT_AHEAD = 3
 WARM_BEFORE = 5
+WARM_LAST = 2
 
 
 def tile_higcin_volleyball_pa_kernel(tc, x, Wtheta, Wphi, out_0, out_1):
@@ -73,22 +77,24 @@ def tile_higcin_volleyball_pa_kernel(tc, x, Wtheta, Wphi, out_0, out_1):
         h_scales = [keep.tile([P, 2 * P], U8, name="h_scales%d" % f, align_bytes=64) for f in range(FRAMES)]
         for f in range(FRAMES):
             nc.vector.memset(h_scales[f][:].bitcast(I32), 0)
-        block_sum = keep.tile([P, GROUP], F32, name="block_sum")
+        block_sum = keep.tile([P, HALF], F32, name="block_sum")
         nc.vector.tensor_reduce(
-            out=block_sum[:], in_=ident[:].rearrange("p (t j) -> p j t", j=GROUP), axis=AX.X, op=ALU.add
+            out=block_sum[:], in_=ident[:].rearrange("p (b j) -> p j b", j=HALF), axis=AX.X, op=ALU.add
         )
-        same_node = keep.tile([P, GROUP], F32, name="same_node")
+        same_node = keep.tile([P, HALF], F32, name="same_node")
         nc.vector.tensor_scalar_mul(out=same_node[:], in0=block_sum[:], scalar1=1.0 / FRAMES)
-        g_codes = keep.tile([P, GROUPS * 2 * P], U32, name="g_codes", align_bytes=64)
-        g_scales = keep.tile([P, GROUPS * 2 * P], U8, name="g_scales", align_bytes=64)
-        g_codes_view = g_codes[:].bitcast(I32).rearrange("p (g w t j) -> p w g t j", g=GROUPS, w=2, t=FRAMES)
-        g_scales_view = g_scales[:].rearrange("p (g w t j) -> p w g t j", g=GROUPS, w=2, t=FRAMES)
-        masked = keep.tile([P, GROUPS * FRAMES, GROUP], F32, name="masked")
+        g_codes = keep.tile([P, GROUPS * 8 * CHUNK], U32, name="g_codes", align_bytes=64)
+        g_scales = keep.tile([P, GROUPS * 8 * CHUNK], U8, name="g_scales", align_bytes=64)
+        g_codes_view = g_codes[:].bitcast(I32).rearrange("p (g c z t j) -> p z g c t j", g=GROUPS, c=4, z=2, t=FRAMES)
+        g_scales_view = g_scales[:].rearrange("p (g c z t j) -> p z g c t j", g=GROUPS, c=4, z=2, t=FRAMES)
+        for plane, words in ((g_codes, CHUNK), (g_scales, CHUNK // 4)):
+            nc.gpsimd.memset(plane[:].bitcast(I32).rearrange("p (gc z n) -> p z gc n", z=2, n=words)[:, 1], 0)
+        masked = keep.tile([P, GROUPS * FRAMES, HALF], F32, name="masked")
         tw_rows = keep.tile([P, GROUPS * FRAMES], F32, name="tw_rows")
         warm_bank = first_bank.tile([P, BANK], F32, tag="first", name="warm_bank")
 
-        def warm_up():
-            nc.tensor.matmul(out=warm_bank[:], lhsT=zeros[:, 0:P], rhs=zeros[:], start=True, stop=True)
+        def warm_up(bank):
+            nc.tensor.matmul(out=bank[:], lhsT=zeros[:, 0:P], rhs=zeros[:], start=True, stop=True)
 
         ordered = {}
         waiting = []
@@ -118,7 +124,7 @@ def tile_higcin_volleyball_pa_kernel(tc, x, Wtheta, Wphi, out_0, out_1):
                     for h in range(2):
                         nc.tensor.transpose(bank[:, c, h, :], words[:, c, h, :], ident[:])
                 if warm:
-                    warm_up()
+                    warm_up(warm_bank)
                 grouped = stage.tile([P, FEATURES], BF16, tag="grouped", name="grouped", align_bytes=64)
                 target = grouped[:].bitcast(F32).rearrange("p (c r h) -> p c r h", c=PASSES, h=2)
                 source = bank[:].rearrange("p c h r -> p c r h")
@@ -176,10 +182,11 @@ def tile_higcin_volleyball_pa_kernel(tc, x, Wtheta, Wphi, out_0, out_1):
                 return
             f, w_from, w_to = unmoved["piece"]
             cols = slice(w_from * P, w_to * P)
+            chunks = slice(w_from * HALVES, w_to * HALVES)
             for plain, by_group in ((h_codes[f][:].bitcast(I32), g_codes_view), (h_scales[f][:], g_scales_view)):
                 nc.vector.tensor_copy(
-                    out=by_group[:, w_from:w_to, :, f, :],
-                    in_=plain[:, cols].rearrange("p (w j g) -> p w g j", j=GROUP, g=GROUPS),
+                    out=by_group[:, 0, :, chunks, f, :],
+                    in_=plain[:, cols].rearrange("p (c j g) -> p g c j", j=HALF, g=GROUPS),
                 )
 
         def spatial(bank, f):
@@ -199,31 +206,36 @@ def tile_higcin_volleyball_pa_kernel(tc, x, Wtheta, Wphi, out_0, out_1):
             nc.scalar.mul(out=sw_rows[:, used, :], in_=bank[:, used, :], mul=1.0 / P)
             nc.sync.dma_start(out=out_0[0, f_from:f_to].rearrange("t j k -> j t k"), in_=sw_rows[:, used, :])
 
-        def temporal(half):
-            bank = flip_banks.tile([P, 4, P], F32, tag="flip", name="bank")
-            for i in range(4):
-                first = (4 * half + i) * 2 * P
+        def temporal(bank, g):
+            first = g * 8 * CHUNK
+            for h in range(HALVES):
+                still = slice(first + h * CHUNK, first + h * CHUNK + P)
+                moving = slice(first + (4 + 2 * h) * CHUNK, first + (4 + 2 * h) * CHUNK + P)
                 nc.tensor.matmul_mx(
-                    out=bank[:, i, :],
-                    lhsT=g_codes[:, first : first + P].bitcast(FP8X4),
-                    lhsT_scale=g_scales[:, first : first + P],
-                    rhs=g_codes[:, first + P : first + 2 * P].bitcast(FP8X4),
-                    rhs_scale=g_scales[:, first + P : first + 2 * P],
-                    start=True,
-                    stop=True,
+                    out=bank[:, g % 2, :],
+                    lhsT=g_codes[:, still].bitcast(FP8X4),
+                    lhsT_scale=g_scales[:, still],
+                    rhs=g_codes[:, moving].bitcast(FP8X4),
+                    rhs_scale=g_scales[:, moving],
+                    start=(h == 0),
+                    stop=(h == HALVES - 1),
                 )
-            return bank
 
-        def keep_same_node(bank, half):
+        def keep_same_node(bank, g_from, g_to):
+            count = g_to - g_from
             nc.vector.tensor_tensor(
-                out=masked[:, 32 * half : 32 * half + 32, :],
-                in0=bank[:].rearrange("p g (s j) -> p (g s) j", j=GROUP),
-                in1=same_node[:].unsqueeze(1).to_broadcast([P, 32, GROUP]),
+                out=masked[:, g_from * FRAMES : g_to * FRAMES, :].rearrange("p (g s) j -> p g s j", s=FRAMES),
+                in0=bank[:, :, 0:CHUNK].rearrange("p g (s j) -> p g s j", j=HALF),
+                in1=same_node[:].unsqueeze(1).unsqueeze(1).to_broadcast([P, count, FRAMES, HALF]),
                 op=ALU.mult,
             )
 
+        def sum_nodes(g_from, g_to):
+            pairs = slice(g_from * FRAMES, g_to * FRAMES)
+            nc.vector.tensor_reduce(out=tw_rows[:, pairs], in_=masked[:, pairs, :], axis=AX.X, op=ALU.add)
+
         for i in range(WARM_BEFORE):
-            warm_up()
+            warm_up(warm_bank)
         transpose_run(theta_tiles)
         transpose_run(x_tiles[0:3], warm=True)
         transpose_run(phi_tiles[0:1])
@@ -249,15 +261,21 @@ def tile_higcin_volleyball_pa_kernel(tc, x, Wtheta, Wphi, out_0, out_1):
         for f in range(4, FRAMES - 1):
             spatial(sw_late, f)
         store_spatial(sw_late, 4, FRAMES - 1)
+        for i in range(WARM_LAST):
+            warm_up(flip_banks.tile([P, BANK], F32, tag="flip", name="idle_bank"))
         spatial(sw_last, FRAMES - 1)
         store_spatial(sw_last, FRAMES - 1, FRAMES)
-        tw_banks = [temporal(0), temporal(1)]
-        keep_same_node(tw_banks[0], 0)
-        keep_same_node(tw_banks[1], 1)
-        for half in range(2):
-            pairs = slice(32 * half, 32 * half + 32)
-            nc.vector.tensor_reduce(out=tw_rows[:, pairs], in_=masked[:, pairs, :], axis=AX.X, op=ALU.add)
+        tw_banks = [flip_banks.tile([P, 2, P], F32, tag="flip", name="tw_bank") for pair in range(3)]
+        tw_banks.append(proj_banks.tile([P, 2, P], F32, tag="proj", name="tw_bank"))
+        for g in range(GROUPS):
+            temporal(tw_banks[g // 2], g)
+        for pair in range(5):
+            if pair < 4:
+                keep_same_node(tw_banks[pair], 2 * pair, 2 * pair + 2)
+            if pair > 0:
+                sum_nodes(2 * pair - 2, 2 * pair)
+        for h in range(HALVES):
             nc.sync.dma_start(
-                out=out_1[0].rearrange("t n s -> (t n) s").rearrange("(p g) s -> p (g s)", g=GROUPS)[:, pairs],
-                in_=tw_rows[:, pairs],
+                out=out_1[0].rearrange("t (h j g) s -> h t j (g s)", h=HALVES, j=HALF)[h],
+                in_=tw_rows[h * CHUNK : (h + 1) * CHUNK, :],
             )

@@ -29,7 +29,7 @@ PHI = 1
 FLOPS = 2 * (FRAMES * P) * FEATURES * (2 * LATENT) + 2 * FRAMES * P * P * LATENT + 2 * P * FRAMES * FRAMES * LATENT
 
 VECTOR_EMPTIES = (("x", 5), ("x", 6))
-UNSORTED = 6
+UNSORTED = 4
 SORT_AHEAD = 3
 WARM_BEFORE = 5
 WARM_LAST = 2
@@ -87,6 +87,9 @@ def tile_higcin_volleyball_pa_kernel(tc, x, Wtheta, Wphi, out_0, out_1):
         g_scales = keep.tile([P, GROUPS * 8 * CHUNK], U8, name="g_scales", align_bytes=64)
         g_codes_view = g_codes[:].bitcast(I32).rearrange("p (g c z t j) -> p z g c t j", g=GROUPS, c=4, z=2, t=FRAMES)
         g_scales_view = g_scales[:].rearrange("p (g c z t j) -> p z g c t j", g=GROUPS, c=4, z=2, t=FRAMES)
+        g_scale_words_view = (
+            g_scales[:].bitcast(I32).rearrange("p (g c z t j) -> p z g c t j", g=GROUPS, c=4, z=2, t=FRAMES)
+        )
         for plane, words in ((g_codes, CHUNK), (g_scales, CHUNK // 4)):
             nc.gpsimd.memset(plane[:].bitcast(I32).rearrange("p (gc z n) -> p z gc n", z=2, n=words)[:, 1], 0)
         masked = keep.tile([P, GROUPS * FRAMES, HALF], F32, name="masked")
@@ -160,7 +163,13 @@ def tile_higcin_volleyball_pa_kernel(tc, x, Wtheta, Wphi, out_0, out_1):
                         )
                 if f not in h_grouped:
                     h_grouped[f] = stage.tile([P, 2, P, PACK], BF16, tag="h_grouped", name="h_grouped", align_bytes=64)
-                nc.scalar.copy(out=h_grouped[f][:, w, :, :], in_=bank[:].rearrange("p i r -> p r i"))
+                if w == THETA:
+                    nc.scalar.copy(out=h_grouped[f][:, w, :, :], in_=bank[:].rearrange("p i r -> p r i"))
+                else:
+                    nc.scalar.copy(
+                        out=h_grouped[f][:, w, :, :].rearrange("p (g n) i -> p g n i", g=GROUPS),
+                        in_=bank[:].rearrange("p i (n g) -> p g n i", g=GROUPS),
+                    )
                 if f == FRAMES - 1:
                     waiting.append((quantise_h, f, w, w + 1))
                 elif w == PHI:
@@ -181,13 +190,20 @@ def tile_higcin_volleyball_pa_kernel(tc, x, Wtheta, Wphi, out_0, out_1):
             if "piece" not in unmoved:
                 return
             f, w_from, w_to = unmoved["piece"]
-            cols = slice(w_from * P, w_to * P)
-            chunks = slice(w_from * HALVES, w_to * HALVES)
-            for plain, by_group in ((h_codes[f][:].bitcast(I32), g_codes_view), (h_scales[f][:], g_scales_view)):
-                nc.vector.tensor_copy(
-                    out=by_group[:, 0, :, chunks, f, :],
-                    in_=plain[:, cols].rearrange("p (c j g) -> p g c j", j=HALF, g=GROUPS),
-                )
+            if w_from == THETA:
+                for plain, by_group in ((h_codes[f][:].bitcast(I32), g_codes_view), (h_scales[f][:], g_scales_view)):
+                    nc.vector.tensor_copy(
+                        out=by_group[:, 0, :, 0:HALVES, f, :],
+                        in_=plain[:, 0:P].rearrange("p (h j g) -> p g h j", h=HALVES, g=GROUPS),
+                    )
+            if w_to == PHI + 1:
+                for plain, nodes, by_group in ((h_codes[f], 1, g_codes_view), (h_scales[f], 4, g_scale_words_view)):
+                    nc.vector.tensor_copy(
+                        out=by_group[:, 0, :, HALVES : 2 * HALVES, f, :],
+                        in_=plain[:]
+                        .bitcast(I32)[:, P // nodes : 2 * P // nodes]
+                        .rearrange("p (g h j) -> p g h j", g=GROUPS, h=HALVES),
+                    )
 
         def spatial(bank, f):
             nc.tensor.matmul_mx(
@@ -203,7 +219,11 @@ def tile_higcin_volleyball_pa_kernel(tc, x, Wtheta, Wphi, out_0, out_1):
         def store_spatial(bank, f_from, f_to):
             sw_rows = stage.tile([P, 4, P], F32, tag="sw_rows", name="sw_rows")
             used = slice(f_from % 4, (f_to - 1) % 4 + 1)
-            nc.scalar.mul(out=sw_rows[:, used, :], in_=bank[:, used, :], mul=1.0 / P)
+            nc.scalar.mul(
+                out=sw_rows[:, used, :].rearrange("p f (n g) -> p f n g", g=GROUPS),
+                in_=bank[:, used, :].rearrange("p f (g n) -> p f n g", g=GROUPS),
+                mul=1.0 / P,
+            )
             nc.sync.dma_start(out=out_0[0, f_from:f_to].rearrange("t j k -> j t k"), in_=sw_rows[:, used, :])
 
         def temporal(bank, g):
@@ -236,19 +256,16 @@ def tile_higcin_volleyball_pa_kernel(tc, x, Wtheta, Wphi, out_0, out_1):
 
         for i in range(WARM_BEFORE):
             warm_up(warm_bank)
-        transpose_run(theta_tiles)
-        transpose_run(x_tiles[0:3], warm=True)
-        transpose_run(phi_tiles[0:1])
+        transpose_run(theta_tiles + x_tiles[0:2], warm=True)
+        transpose_run(x_tiles[2:3] + phi_tiles[0:2])
         project_run([(0, THETA)])
-        transpose_run(phi_tiles[1:3])
-        project_run([(1, THETA)])
-        transpose_run(phi_tiles[3:4] + x_tiles[3:4])
-        project_run([(2, THETA)])
+        transpose_run(phi_tiles[2:4] + x_tiles[3:4])
+        project_run([(1, THETA), (2, THETA)])
         transpose_run(x_tiles[4:6])
-        project_run([(0, PHI), (3, THETA), (1, PHI)])
+        project_run([(0, PHI), (1, PHI), (3, THETA)])
         transpose_run(x_tiles[6:8])
-        project_run([(2, PHI), (4, THETA), (3, PHI), (4, PHI)])
-        project_run([(f, w) for f in range(5, FRAMES) for w in (THETA, PHI)])
+        project_run([(2, PHI), (3, PHI)])
+        project_run([(f, w) for f in range(4, FRAMES) for w in (THETA, PHI)])
         quantise_waiting(0)
         move_unmoved()
 

@@ -29,6 +29,7 @@ PHI = 1
 FLOPS = 2 * (FRAMES * P) * FEATURES * (2 * LATENT) + 2 * FRAMES * P * P * LATENT + 2 * P * FRAMES * FRAMES * LATENT
 
 VECTOR_EMPTIES = (("x", 5), ("x", 6))
+VECTOR_LOWERS = ((1, THETA),)
 UNSORTED = 4
 SORT_AHEAD = 3
 WARM_BEFORE = 5
@@ -42,8 +43,7 @@ def tile_higcin_volleyball_pa_kernel(tc, x, Wtheta, Wphi, out_0, out_1):
         raw = ctx.enter_context(tc.tile_pool(name="raw", bufs=1))
         keep = ctx.enter_context(tc.tile_pool(name="keep", bufs=1))
         stage = ctx.enter_context(tc.tile_pool(name="stage", bufs=6))
-        flip_banks = ctx.enter_context(tc.psum_pool(name="flip", bufs=3))
-        proj_banks = ctx.enter_context(tc.psum_pool(name="proj", bufs=4))
+        banks = ctx.enter_context(tc.psum_pool(name="banks", bufs=7))
         first_bank = ctx.enter_context(tc.psum_pool(name="first", bufs=1))
 
         theta_tiles = [("theta", i) for i in range(PACK)]
@@ -119,7 +119,7 @@ def tile_higcin_volleyball_pa_kernel(tc, x, Wtheta, Wphi, out_0, out_1):
                 for ahead in tiles[max(place, UNSORTED) : place + SORT_AHEAD + 1]:
                     if ahead not in ordered:
                         sort_words(ahead)
-                bank = flip_banks.tile([P, PASSES, 2, P], F32, tag="flip", name="bank")
+                bank = banks.tile([P, PASSES, 2, P], F32, tag="bank", name="bank")
                 words = rows[key][:].bitcast(F32).rearrange("p (c r h) -> p c h r", c=PASSES, h=2)
                 if key in ordered:
                     words = ordered[key][:]
@@ -147,7 +147,7 @@ def tile_higcin_volleyball_pa_kernel(tc, x, Wtheta, Wphi, out_0, out_1):
 
         def project_run(pairs):
             for f, w in pairs:
-                bank = proj_banks.tile([P, PACK, P], F32, tag="proj", name="bank")
+                bank = banks.tile([P, PACK, P], F32, tag="bank", name="bank")
                 for i in range(PACK):
                     weight = (("theta", i), ("phi", i))[w]
                     for c in range(PASSES):
@@ -163,13 +163,16 @@ def tile_higcin_volleyball_pa_kernel(tc, x, Wtheta, Wphi, out_0, out_1):
                         )
                 if f not in h_grouped:
                     h_grouped[f] = stage.tile([P, 2, P, PACK], BF16, tag="h_grouped", name="h_grouped", align_bytes=64)
-                if w == THETA:
-                    nc.scalar.copy(out=h_grouped[f][:, w, :, :], in_=bank[:].rearrange("p i r -> p r i"))
+                target = h_grouped[f][:, w, :, :]
+                source = bank[:].rearrange("p i r -> p r i")
+                if w == PHI:
+                    target = target.rearrange("p (g n) i -> p g n i", g=GROUPS)
+                    source = bank[:].rearrange("p i (n g) -> p g n i", g=GROUPS)
+                if (f, w) in VECTOR_LOWERS:
+                    quantise_waiting(0)
+                    nc.vector.tensor_copy(out=target, in_=source)
                 else:
-                    nc.scalar.copy(
-                        out=h_grouped[f][:, w, :, :].rearrange("p (g n) i -> p g n i", g=GROUPS),
-                        in_=bank[:].rearrange("p i (n g) -> p g n i", g=GROUPS),
-                    )
+                    nc.scalar.copy(out=target, in_=source)
                 if f == FRAMES - 1:
                     waiting.append((quantise_h, f, w, w + 1))
                 elif w == PHI:
@@ -270,8 +273,8 @@ def tile_higcin_volleyball_pa_kernel(tc, x, Wtheta, Wphi, out_0, out_1):
         move_unmoved()
 
         sw_early = first_bank.tile([P, 4, P], F32, tag="first", name="sw_early")
-        sw_late = proj_banks.tile([P, 4, P], F32, tag="proj", name="sw_late")
-        sw_last = proj_banks.tile([P, 4, P], F32, tag="proj", name="sw_last")
+        sw_late = banks.tile([P, 4, P], F32, tag="bank", name="sw_late")
+        sw_last = banks.tile([P, 4, P], F32, tag="bank", name="sw_last")
         for f in range(4):
             spatial(sw_early, f)
         store_spatial(sw_early, 0, 4)
@@ -279,11 +282,11 @@ def tile_higcin_volleyball_pa_kernel(tc, x, Wtheta, Wphi, out_0, out_1):
             spatial(sw_late, f)
         store_spatial(sw_late, 4, FRAMES - 1)
         for i in range(WARM_LAST):
-            warm_up(flip_banks.tile([P, BANK], F32, tag="flip", name="idle_bank"))
+            warm_up(banks.tile([P, BANK], F32, tag="bank", name="idle_bank"))
         spatial(sw_last, FRAMES - 1)
         store_spatial(sw_last, FRAMES - 1, FRAMES)
-        tw_banks = [flip_banks.tile([P, 2, P], F32, tag="flip", name="tw_bank") for pair in range(3)]
-        tw_banks.append(proj_banks.tile([P, 2, P], F32, tag="proj", name="tw_bank"))
+        tw_banks = [banks.tile([P, 2, P], F32, tag="bank", name="tw_bank") for pair in range(3)]
+        tw_banks.append(banks.tile([P, 2, P], F32, tag="bank", name="tw_bank"))
         for g in range(GROUPS):
             temporal(tw_banks[g // 2], g)
         for pair in range(5):
@@ -291,8 +294,8 @@ def tile_higcin_volleyball_pa_kernel(tc, x, Wtheta, Wphi, out_0, out_1):
                 keep_same_node(tw_banks[pair], 2 * pair, 2 * pair + 2)
             if pair > 0:
                 sum_nodes(2 * pair - 2, 2 * pair)
-        for h in range(HALVES):
-            nc.sync.dma_start(
+        for h, queue in enumerate((nc.sync, nc.scalar)):
+            queue.dma_start(
                 out=out_1[0].rearrange("t (h j g) s -> h t j (g s)", h=HALVES, j=HALF)[h],
                 in_=tw_rows[h * CHUNK : (h + 1) * CHUNK, :],
             )

@@ -30,9 +30,10 @@ FLOPS = 2 * (FRAMES * P) * FEATURES * (2 * LATENT) + 2 * FRAMES * P * P * LATENT
 
 VECTOR_EMPTIES = (("x", 5), ("x", 6))
 VECTOR_LOWERS = ((1, THETA),)
-UNSORTED = 4
+UNSORTED = (("theta", 0), ("theta", 1), ("x", 1), ("x", 2))
 SORT_AHEAD = 3
 WARM_BEFORE = 5
+WARM_BEHIND = (("theta", 0), ("theta", 1), ("theta", 2), ("theta", 3), ("x", 1), ("x", 2))
 WARM_LAST = 2
 
 
@@ -113,11 +114,11 @@ def tile_higcin_volleyball_pa_kernel(tc, x, Wtheta, Wphi, out_0, out_1):
                 out=ordered[key][:], in_=rows[key][:].bitcast(F32).rearrange("p (c r h) -> p c h r", c=PASSES, h=2)
             )
 
-        def transpose_run(keys, warm=False):
+        def transpose_run(keys):
             for key in keys:
                 place = tiles.index(key)
-                for ahead in tiles[max(place, UNSORTED) : place + SORT_AHEAD + 1]:
-                    if ahead not in ordered:
+                for ahead in tiles[place : place + SORT_AHEAD + 1]:
+                    if ahead not in ordered and ahead not in UNSORTED:
                         sort_words(ahead)
                 bank = banks.tile([P, PASSES, 2, P], F32, tag="bank", name="bank")
                 words = rows[key][:].bitcast(F32).rearrange("p (c r h) -> p c h r", c=PASSES, h=2)
@@ -126,7 +127,7 @@ def tile_higcin_volleyball_pa_kernel(tc, x, Wtheta, Wphi, out_0, out_1):
                 for c in range(PASSES):
                     for h in range(2):
                         nc.tensor.transpose(bank[:, c, h, :], words[:, c, h, :], ident[:])
-                if warm:
+                if key in WARM_BEHIND:
                     warm_up(warm_bank)
                 grouped = stage.tile([P, FEATURES], BF16, tag="grouped", name="grouped", align_bytes=64)
                 target = grouped[:].bitcast(F32).rearrange("p (c r h) -> p c r h", c=PASSES, h=2)
@@ -259,8 +260,7 @@ def tile_higcin_volleyball_pa_kernel(tc, x, Wtheta, Wphi, out_0, out_1):
 
         for i in range(WARM_BEFORE):
             warm_up(warm_bank)
-        transpose_run(theta_tiles + x_tiles[0:2], warm=True)
-        transpose_run(x_tiles[2:3] + phi_tiles[0:2])
+        transpose_run(theta_tiles + x_tiles[0:3] + phi_tiles[0:2])
         project_run([(0, THETA)])
         transpose_run(phi_tiles[2:4] + x_tiles[3:4])
         project_run([(1, THETA), (2, THETA)])

@@ -24,6 +24,9 @@ GROUPS = P // GROUP
 HALVES = 2
 HALF = GROUP // HALVES
 CHUNK = FRAMES * HALF
+CHUNKS = 5
+ZEROS = 1
+FIRST_PHI = 3
 THETA = 0
 PHI = 1
 FLOPS = 2 * (FRAMES * P) * FEATURES * (2 * LATENT) + 2 * FRAMES * P * P * LATENT + 2 * P * FRAMES * FRAMES * LATENT
@@ -84,15 +87,17 @@ def tile_higcin_volleyball_pa_kernel(tc, x, Wtheta, Wphi, out_0, out_1):
         )
         same_node = keep.tile([P, HALF], F32, name="same_node")
         nc.vector.tensor_scalar_mul(out=same_node[:], in0=block_sum[:], scalar1=1.0 / FRAMES)
-        g_codes = keep.tile([P, GROUPS * 8 * CHUNK], U32, name="g_codes", align_bytes=64)
-        g_scales = keep.tile([P, GROUPS * 8 * CHUNK], U8, name="g_scales", align_bytes=64)
-        g_codes_view = g_codes[:].bitcast(I32).rearrange("p (g c z t j) -> p z g c t j", g=GROUPS, c=4, z=2, t=FRAMES)
-        g_scales_view = g_scales[:].rearrange("p (g c z t j) -> p z g c t j", g=GROUPS, c=4, z=2, t=FRAMES)
-        g_scale_words_view = (
-            g_scales[:].bitcast(I32).rearrange("p (g c z t j) -> p z g c t j", g=GROUPS, c=4, z=2, t=FRAMES)
-        )
-        for plane, words in ((g_codes, CHUNK), (g_scales, CHUNK // 4)):
-            nc.gpsimd.memset(plane[:].bitcast(I32).rearrange("p (gc z n) -> p z gc n", z=2, n=words)[:, 1], 0)
+        g_codes = keep.tile([P, GROUPS * CHUNKS * CHUNK + CHUNK], U32, name="g_codes", align_bytes=64)
+        g_scales = keep.tile([P, GROUPS * CHUNKS * CHUNK + CHUNK], U8, name="g_scales", align_bytes=64)
+        in_groups = slice(0, GROUPS * CHUNKS * CHUNK)
+        by_chunk = "p (g c t j) -> p g c t j"
+        g_codes_view = g_codes[:, in_groups].bitcast(I32).rearrange(by_chunk, g=GROUPS, c=CHUNKS, t=FRAMES)
+        g_scales_view = g_scales[:, in_groups].rearrange(by_chunk, g=GROUPS, c=CHUNKS, t=FRAMES)
+        g_scale_words_view = g_scales[:, in_groups].bitcast(I32).rearrange(by_chunk, g=GROUPS, c=CHUNKS, t=FRAMES)
+        for plane in (g_codes, g_scales):
+            groups_words = plane[:, in_groups].bitcast(I32).rearrange("p (g c n) -> p g c n", g=GROUPS, c=CHUNKS)
+            nc.vector.memset(groups_words[:, :, ZEROS, :], 0)
+            nc.vector.memset(plane[:, GROUPS * CHUNKS * CHUNK :].bitcast(I32), 0)
         masked = keep.tile([P, GROUPS * FRAMES, HALF], F32, name="masked")
         tw_rows = keep.tile([P, GROUPS * FRAMES], F32, name="tw_rows")
         warm_bank = first_bank.tile([P, BANK], F32, tag="first", name="warm_bank")
@@ -197,13 +202,13 @@ def tile_higcin_volleyball_pa_kernel(tc, x, Wtheta, Wphi, out_0, out_1):
             if w_from == THETA:
                 for plain, by_group in ((h_codes[f][:].bitcast(I32), g_codes_view), (h_scales[f][:], g_scales_view)):
                     nc.vector.tensor_copy(
-                        out=by_group[:, 0, :, 0:HALVES, f, :],
+                        out=by_group[:, :, 0:FIRST_PHI:2, f, :],
                         in_=plain[:, 0:P].rearrange("p (h j g) -> p g h j", h=HALVES, g=GROUPS),
                     )
             if w_to == PHI + 1:
                 for plain, nodes, by_group in ((h_codes[f], 1, g_codes_view), (h_scales[f], 4, g_scale_words_view)):
                     nc.vector.tensor_copy(
-                        out=by_group[:, 0, :, HALVES : 2 * HALVES, f, :],
+                        out=by_group[:, :, FIRST_PHI:CHUNKS, f, :],
                         in_=plain[:]
                         .bitcast(I32)[:, P // nodes : 2 * P // nodes]
                         .rearrange("p (g h j) -> p g h j", g=GROUPS, h=HALVES),
@@ -231,10 +236,10 @@ def tile_higcin_volleyball_pa_kernel(tc, x, Wtheta, Wphi, out_0, out_1):
             nc.sync.dma_start(out=out_0[0, f_from:f_to].rearrange("t j k -> j t k"), in_=sw_rows[:, used, :])
 
         def temporal(bank, g):
-            first = g * 8 * CHUNK
+            first = g * CHUNKS * CHUNK
             for h in range(HALVES):
                 still = slice(first + h * CHUNK, first + h * CHUNK + P)
-                moving = slice(first + (4 + 2 * h) * CHUNK, first + (4 + 2 * h) * CHUNK + P)
+                moving = slice(first + (FIRST_PHI + h) * CHUNK, first + (FIRST_PHI + h) * CHUNK + P)
                 nc.tensor.matmul_mx(
                     out=bank[:, g % 2, :],
                     lhsT=g_codes[:, still].bitcast(FP8X4),

@@ -25,8 +25,9 @@ HALVES = 2
 HALF = GROUP // HALVES
 CHUNK = FRAMES * HALF
 CHUNKS = 5
-ZEROS = 1
-FIRST_PHI = 3
+FIRST_THETA = 2
+ZEROS = 3
+SINGLE_FROM = 6
 THETA = 0
 PHI = 1
 FLOPS = 2 * (FRAMES * P) * FEATURES * (2 * LATENT) + 2 * FRAMES * P * P * LATENT + 2 * P * FRAMES * FRAMES * LATENT
@@ -77,18 +78,17 @@ def tile_higcin_volleyball_pa_kernel(tc, x, Wtheta, Wphi, out_0, out_1):
         nc.scalar.mul(out=table_load[:], in_=zeros[:, 0:1], mul=1.0)
         ident = keep.tile([P, P], F32, name="ident")
         make_identity(nc, ident[:])
-        h_codes = [keep.tile([P, 2 * P], U32, name="h_codes%d" % f, align_bytes=64) for f in range(FRAMES)]
-        h_scales = [keep.tile([P, 2 * P], U8, name="h_scales%d" % f, align_bytes=64) for f in range(FRAMES)]
-        for f in range(FRAMES):
-            nc.vector.memset(h_scales[f][:].bitcast(I32), 0)
+        h_codes = keep.tile([P, FRAMES, 2 * P], U32, name="h_codes", align_bytes=64)
+        h_scales = keep.tile([P, FRAMES, 2 * P], U8, name="h_scales", align_bytes=64)
+        nc.vector.memset(h_scales[:].rearrange("p f n -> p (f n)").bitcast(I32), 0)
         block_sum = keep.tile([P, HALF], F32, name="block_sum")
         nc.vector.tensor_reduce(
             out=block_sum[:], in_=ident[:].rearrange("p (b j) -> p j b", j=HALF), axis=AX.X, op=ALU.add
         )
         same_node = keep.tile([P, HALF], F32, name="same_node")
         nc.vector.tensor_scalar_mul(out=same_node[:], in0=block_sum[:], scalar1=1.0 / FRAMES)
-        g_codes = keep.tile([P, GROUPS * CHUNKS * CHUNK + CHUNK], U32, name="g_codes", align_bytes=64)
-        g_scales = keep.tile([P, GROUPS * CHUNKS * CHUNK + CHUNK], U8, name="g_scales", align_bytes=64)
+        g_codes = keep.tile([P, GROUPS * CHUNKS * CHUNK], U32, name="g_codes", align_bytes=64)
+        g_scales = keep.tile([P, GROUPS * CHUNKS * CHUNK], U8, name="g_scales", align_bytes=64)
         in_groups = slice(0, GROUPS * CHUNKS * CHUNK)
         by_chunk = "p (g c t j) -> p g c t j"
         g_codes_view = g_codes[:, in_groups].bitcast(I32).rearrange(by_chunk, g=GROUPS, c=CHUNKS, t=FRAMES)
@@ -97,7 +97,6 @@ def tile_higcin_volleyball_pa_kernel(tc, x, Wtheta, Wphi, out_0, out_1):
         for plane in (g_codes, g_scales):
             groups_words = plane[:, in_groups].bitcast(I32).rearrange("p (g c n) -> p g c n", g=GROUPS, c=CHUNKS)
             nc.vector.memset(groups_words[:, :, ZEROS, :], 0)
-            nc.vector.memset(plane[:, GROUPS * CHUNKS * CHUNK :].bitcast(I32), 0)
         masked = keep.tile([P, GROUPS * FRAMES, HALF], F32, name="masked")
         tw_rows = keep.tile([P, GROUPS * FRAMES], F32, name="tw_rows")
         warm_bank = first_bank.tile([P, BANK], F32, tag="first", name="warm_bank")
@@ -179,7 +178,7 @@ def tile_higcin_volleyball_pa_kernel(tc, x, Wtheta, Wphi, out_0, out_1):
                     nc.vector.tensor_copy(out=target, in_=source)
                 else:
                     nc.scalar.copy(out=target, in_=source)
-                if f == FRAMES - 1:
+                if f >= SINGLE_FROM:
                     waiting.append((quantise_h, f, w, w + 1))
                 elif w == PHI:
                     waiting.append((quantise_h, f, THETA, PHI + 1))
@@ -188,39 +187,41 @@ def tile_higcin_volleyball_pa_kernel(tc, x, Wtheta, Wphi, out_0, out_1):
         def quantise_h(f, w_from, w_to):
             cols = slice(w_from * P, w_to * P)
             nc.vector.quantize_mx(
-                out=h_codes[f][:, cols].bitcast(FP8X4),
-                scales=h_scales[f][:, cols],
+                out=h_codes[:, f, cols].bitcast(FP8X4),
+                scales=h_scales[:, f, cols],
                 in_=h_grouped[f][:, w_from:w_to, :, :].rearrange("p w r i -> p (w r i)"),
             )
             move_unmoved()
-            unmoved["piece"] = (f, w_from, w_to)
+            unmoved["piece"] = (f, f + 1, w_from, w_to)
+            if (f, w_from) == (FRAMES - 1, THETA):
+                move_unmoved()
 
         def move_unmoved():
             if "piece" not in unmoved:
                 return
-            f, w_from, w_to = unmoved["piece"]
+            f_from, f_to, w_from, w_to = unmoved.pop("piece")
             if w_from == THETA:
-                for plain, by_group in ((h_codes[f][:].bitcast(I32), g_codes_view), (h_scales[f][:], g_scales_view)):
+                for plain, by_group in ((h_codes[:].bitcast(I32), g_codes_view), (h_scales[:], g_scales_view)):
                     nc.vector.tensor_copy(
-                        out=by_group[:, :, 0:FIRST_PHI:2, f, :],
-                        in_=plain[:, 0:P].rearrange("p (h j g) -> p g h j", h=HALVES, g=GROUPS),
+                        out=by_group[:, :, FIRST_THETA:CHUNKS:2, f_from:f_to, :],
+                        in_=plain[:, f_from:f_to, 0:P].rearrange("p t (h j g) -> p g h t j", h=HALVES, g=GROUPS),
                     )
             if w_to == PHI + 1:
-                for plain, nodes, by_group in ((h_codes[f], 1, g_codes_view), (h_scales[f], 4, g_scale_words_view)):
+                for plain, nodes, by_group in ((h_codes, 1, g_codes_view), (h_scales, 4, g_scale_words_view)):
                     nc.vector.tensor_copy(
-                        out=by_group[:, :, FIRST_PHI:CHUNKS, f, :],
-                        in_=plain[:]
-                        .bitcast(I32)[:, P // nodes : 2 * P // nodes]
-                        .rearrange("p (g h j) -> p g h j", g=GROUPS, h=HALVES),
+                        out=by_group[:, :, 0:HALVES, f_from:f_to, :],
+                        in_=plain[:, f_from:f_to, :]
+                        .bitcast(I32)[:, :, P // nodes : 2 * P // nodes]
+                        .rearrange("p t (g h j) -> p g h t j", g=GROUPS, h=HALVES),
                     )
 
         def spatial(bank, f):
             nc.tensor.matmul_mx(
                 out=bank[:, f % 4, :],
-                lhsT=h_codes[f][:, 0:P].bitcast(FP8X4),
-                lhsT_scale=h_scales[f][:, 0:P],
-                rhs=h_codes[f][:, P : 2 * P].bitcast(FP8X4),
-                rhs_scale=h_scales[f][:, P : 2 * P],
+                lhsT=h_codes[:, f, 0:P].bitcast(FP8X4),
+                lhsT_scale=h_scales[:, f, 0:P],
+                rhs=h_codes[:, f, P : 2 * P].bitcast(FP8X4),
+                rhs_scale=h_scales[:, f, P : 2 * P],
                 start=True,
                 stop=True,
             )
@@ -238,8 +239,8 @@ def tile_higcin_volleyball_pa_kernel(tc, x, Wtheta, Wphi, out_0, out_1):
         def temporal(bank, g):
             first = g * CHUNKS * CHUNK
             for h in range(HALVES):
-                still = slice(first + h * CHUNK, first + h * CHUNK + P)
-                moving = slice(first + (FIRST_PHI + h) * CHUNK, first + (FIRST_PHI + h) * CHUNK + P)
+                still = slice(first + (FIRST_THETA + h) * CHUNK, first + (FIRST_THETA + h) * CHUNK + P)
+                moving = slice(first + h * CHUNK, first + h * CHUNK + P)
                 nc.tensor.matmul_mx(
                     out=bank[:, g % 2, :],
                     lhsT=g_codes[:, still].bitcast(FP8X4),

@@ -24,12 +24,11 @@ GROUPS = P // GROUP
 HALVES = 2
 HALF = GROUP // HALVES
 CHUNK = FRAMES * HALF
-CHUNKS = 5
-FIRST_THETA = 2
-ZEROS = 3
+CHUNKS = 3
+ZEROS = 1
 SINGLE_FROM = 6
-THETA = 0
-PHI = 1
+PHI = 0
+THETA = 1
 FLOPS = 2 * (FRAMES * P) * FEATURES * (2 * LATENT) + 2 * FRAMES * P * P * LATENT + 2 * P * FRAMES * FRAMES * LATENT
 
 VECTOR_EMPTIES = (("x", 5), ("x", 6))
@@ -87,16 +86,14 @@ def tile_higcin_volleyball_pa_kernel(tc, x, Wtheta, Wphi, out_0, out_1):
         )
         same_node = keep.tile([P, HALF], F32, name="same_node")
         nc.vector.tensor_scalar_mul(out=same_node[:], in0=block_sum[:], scalar1=1.0 / FRAMES)
-        g_codes = keep.tile([P, GROUPS * CHUNKS * CHUNK], U32, name="g_codes", align_bytes=64)
-        g_scales = keep.tile([P, GROUPS * CHUNKS * CHUNK], U8, name="g_scales", align_bytes=64)
-        in_groups = slice(0, GROUPS * CHUNKS * CHUNK)
-        by_chunk = "p (g c t j) -> p g c t j"
-        g_codes_view = g_codes[:, in_groups].bitcast(I32).rearrange(by_chunk, g=GROUPS, c=CHUNKS, t=FRAMES)
-        g_scales_view = g_scales[:, in_groups].rearrange(by_chunk, g=GROUPS, c=CHUNKS, t=FRAMES)
-        g_scale_words_view = g_scales[:, in_groups].bitcast(I32).rearrange(by_chunk, g=GROUPS, c=CHUNKS, t=FRAMES)
+        g_codes = keep.tile([P, GROUPS * 2 * CHUNKS * CHUNK], U32, name="g_codes", align_bytes=64)
+        g_scales = keep.tile([P, GROUPS * 2 * CHUNKS * CHUNK], U8, name="g_scales", align_bytes=64)
+        by_chunk = "p (g w c t j) -> p w g c t j"
+        g_views = []
         for plane in (g_codes, g_scales):
-            groups_words = plane[:, in_groups].bitcast(I32).rearrange("p (g c n) -> p g c n", g=GROUPS, c=CHUNKS)
-            nc.vector.memset(groups_words[:, :, ZEROS, :], 0)
+            words = plane[:].bitcast(I32)
+            nc.vector.memset(words.rearrange("p (k c n) -> p k c n", k=GROUPS * 2, c=CHUNKS)[:, :, ZEROS, :], 0)
+            g_views.append(words.rearrange(by_chunk, g=GROUPS, w=2, c=CHUNKS, t=FRAMES))
         masked = keep.tile([P, GROUPS * FRAMES, HALF], F32, name="masked")
         tw_rows = keep.tile([P, GROUPS * FRAMES], F32, name="tw_rows")
         warm_bank = first_bank.tile([P, BANK], F32, tag="first", name="warm_bank")
@@ -154,7 +151,7 @@ def tile_higcin_volleyball_pa_kernel(tc, x, Wtheta, Wphi, out_0, out_1):
             for f, w in pairs:
                 bank = banks.tile([P, PACK, P], F32, tag="bank", name="bank")
                 for i in range(PACK):
-                    weight = (("theta", i), ("phi", i))[w]
+                    weight = (("phi", i), ("theta", i))[w]
                     for c in range(PASSES):
                         cols = slice(c * P, (c + 1) * P)
                         nc.tensor.matmul_mx(
@@ -168,11 +165,8 @@ def tile_higcin_volleyball_pa_kernel(tc, x, Wtheta, Wphi, out_0, out_1):
                         )
                 if f not in h_grouped:
                     h_grouped[f] = stage.tile([P, 2, P, PACK], BF16, tag="h_grouped", name="h_grouped", align_bytes=64)
-                target = h_grouped[f][:, w, :, :]
-                source = bank[:].rearrange("p i r -> p r i")
-                if w == PHI:
-                    target = target.rearrange("p (g n) i -> p g n i", g=GROUPS)
-                    source = bank[:].rearrange("p i (n g) -> p g n i", g=GROUPS)
+                target = h_grouped[f][:, w, :, :].rearrange("p (g n) i -> p g n i", g=GROUPS)
+                source = bank[:].rearrange("p i (n g) -> p g n i", g=GROUPS)
                 if (f, w) in VECTOR_LOWERS:
                     quantise_waiting(0)
                     nc.vector.tensor_copy(out=target, in_=source)
@@ -181,7 +175,7 @@ def tile_higcin_volleyball_pa_kernel(tc, x, Wtheta, Wphi, out_0, out_1):
                 if f >= SINGLE_FROM:
                     waiting.append((quantise_h, f, w, w + 1))
                 elif w == PHI:
-                    waiting.append((quantise_h, f, THETA, PHI + 1))
+                    waiting.append((quantise_h, f, PHI, THETA + 1))
                 quantise_waiting(1)
 
         def quantise_h(f, w_from, w_to):
@@ -192,36 +186,29 @@ def tile_higcin_volleyball_pa_kernel(tc, x, Wtheta, Wphi, out_0, out_1):
                 in_=h_grouped[f][:, w_from:w_to, :, :].rearrange("p w r i -> p (w r i)"),
             )
             move_unmoved()
-            unmoved["piece"] = (f, f + 1, w_from, w_to)
+            unmoved["piece"] = (f, w_from, w_to)
             if (f, w_from) == (FRAMES - 1, THETA):
                 move_unmoved()
 
         def move_unmoved():
             if "piece" not in unmoved:
                 return
-            f_from, f_to, w_from, w_to = unmoved.pop("piece")
-            if w_from == THETA:
-                for plain, by_group in ((h_codes[:].bitcast(I32), g_codes_view), (h_scales[:], g_scales_view)):
-                    nc.vector.tensor_copy(
-                        out=by_group[:, :, FIRST_THETA:CHUNKS:2, f_from:f_to, :],
-                        in_=plain[:, f_from:f_to, 0:P].rearrange("p t (h j g) -> p g h t j", h=HALVES, g=GROUPS),
-                    )
-            if w_to == PHI + 1:
-                for plain, nodes, by_group in ((h_codes, 1, g_codes_view), (h_scales, 4, g_scale_words_view)):
-                    nc.vector.tensor_copy(
-                        out=by_group[:, :, 0:HALVES, f_from:f_to, :],
-                        in_=plain[:, f_from:f_to, :]
-                        .bitcast(I32)[:, :, P // nodes : 2 * P // nodes]
-                        .rearrange("p t (g h j) -> p g h t j", g=GROUPS, h=HALVES),
-                    )
+            f, w_from, w_to = unmoved.pop("piece")
+            for plain, nodes, by_group in ((h_codes, 1, g_views[0]), (h_scales, 4, g_views[1])):
+                nc.vector.tensor_copy(
+                    out=by_group[:, w_from:w_to, :, 0:CHUNKS:2, f, :],
+                    in_=plain[:, f, :]
+                    .bitcast(I32)[:, w_from * P // nodes : w_to * P // nodes]
+                    .rearrange("p (w g h j) -> p w g h j", w=w_to - w_from, g=GROUPS, h=HALVES),
+                )
 
         def spatial(bank, f):
             nc.tensor.matmul_mx(
                 out=bank[:, f % 4, :],
-                lhsT=h_codes[:, f, 0:P].bitcast(FP8X4),
-                lhsT_scale=h_scales[:, f, 0:P],
-                rhs=h_codes[:, f, P : 2 * P].bitcast(FP8X4),
-                rhs_scale=h_scales[:, f, P : 2 * P],
+                lhsT=h_codes[:, f, P : 2 * P].bitcast(FP8X4),
+                lhsT_scale=h_scales[:, f, P : 2 * P],
+                rhs=h_codes[:, f, 0:P].bitcast(FP8X4),
+                rhs_scale=h_scales[:, f, 0:P],
                 start=True,
                 stop=True,
             )
@@ -234,13 +221,16 @@ def tile_higcin_volleyball_pa_kernel(tc, x, Wtheta, Wphi, out_0, out_1):
                 in_=bank[:, used, :].rearrange("p f (g n) -> p f n g", g=GROUPS),
                 mul=1.0 / P,
             )
-            nc.sync.dma_start(out=out_0[0, f_from:f_to].rearrange("t j k -> j t k"), in_=sw_rows[:, used, :])
+            for f in range(f_from, f_to):
+                rows_by_group = out_0[0, f].rearrange("(n g) k -> g n k", g=GROUPS)
+                nc.sync.dma_start(out=rows_by_group, in_=sw_rows[:, f % 4, :])
 
         def temporal(bank, g):
-            first = g * CHUNKS * CHUNK
+            first_phi = (2 * g + PHI) * CHUNKS * CHUNK
+            first_theta = (2 * g + THETA) * CHUNKS * CHUNK
             for h in range(HALVES):
-                still = slice(first + (FIRST_THETA + h) * CHUNK, first + (FIRST_THETA + h) * CHUNK + P)
-                moving = slice(first + h * CHUNK, first + h * CHUNK + P)
+                still = slice(first_theta + h * CHUNK, first_theta + h * CHUNK + P)
+                moving = slice(first_phi + 2 * h * CHUNK, first_phi + 2 * h * CHUNK + P)
                 nc.tensor.matmul_mx(
                     out=bank[:, g % 2, :],
                     lhsT=g_codes[:, still].bitcast(FP8X4),

@@ -165,8 +165,8 @@ def tile_higcin_volleyball_pa_kernel(tc, x, Wtheta, Wphi, out_0, out_1):
                         )
                 if f not in h_grouped:
                     h_grouped[f] = stage.tile([P, 2, P, PACK], BF16, tag="h_grouped", name="h_grouped", align_bytes=64)
-                target = h_grouped[f][:, w, :, :].rearrange("p (g n) i -> p g n i", g=GROUPS)
-                source = bank[:].rearrange("p i (n g) -> p g n i", g=GROUPS)
+                target = h_grouped[f][:, w, :, :].rearrange("p (a j) i -> p a j i", j=HALF)
+                source = bank[:].rearrange("p i (j a) -> p a j i", j=HALF)
                 if (f, w) in VECTOR_LOWERS:
                     quantise_waiting(0)
                     nc.vector.tensor_copy(out=target, in_=source)
@@ -196,10 +196,10 @@ def tile_higcin_volleyball_pa_kernel(tc, x, Wtheta, Wphi, out_0, out_1):
             f, w_from, w_to = unmoved.pop("piece")
             for plain, nodes, by_group in ((h_codes, 1, g_views[0]), (h_scales, 4, g_views[1])):
                 nc.vector.tensor_copy(
-                    out=by_group[:, w_from:w_to, :, 0:CHUNKS:2, f, :],
+                    out=by_group[:, w_from:w_to, :, 0:CHUNKS:2, f, :].rearrange("p w g h j -> p w h g j"),
                     in_=plain[:, f, :]
                     .bitcast(I32)[:, w_from * P // nodes : w_to * P // nodes]
-                    .rearrange("p (w g h j) -> p w g h j", w=w_to - w_from, g=GROUPS, h=HALVES),
+                    .rearrange("p (w h g j) -> p w h g j", w=w_to - w_from, g=GROUPS, h=HALVES),
                 )
 
         def spatial(bank, f):
@@ -217,12 +217,12 @@ def tile_higcin_volleyball_pa_kernel(tc, x, Wtheta, Wphi, out_0, out_1):
             sw_rows = stage.tile([P, 4, P], F32, tag="sw_rows", name="sw_rows")
             used = slice(f_from % 4, (f_to - 1) % 4 + 1)
             nc.scalar.mul(
-                out=sw_rows[:, used, :].rearrange("p f (n g) -> p f n g", g=GROUPS),
-                in_=bank[:, used, :].rearrange("p f (g n) -> p f n g", g=GROUPS),
+                out=sw_rows[:, used, :].rearrange("p f (j a) -> p f j a", j=HALF),
+                in_=bank[:, used, :].rearrange("p f (a j) -> p f j a", j=HALF),
                 mul=1.0 / P,
             )
             for f in range(f_from, f_to):
-                rows_by_group = out_0[0, f].rearrange("(n g) k -> g n k", g=GROUPS)
+                rows_by_group = out_0[0, f].rearrange("(j a) k -> a j k", j=HALF)
                 nc.sync.dma_start(out=rows_by_group, in_=sw_rows[:, f % 4, :])
 
         def temporal(bank, g):
@@ -292,6 +292,6 @@ def tile_higcin_volleyball_pa_kernel(tc, x, Wtheta, Wphi, out_0, out_1):
                 sum_nodes(2 * pair - 2, 2 * pair)
         for h, queue in enumerate((nc.sync, nc.scalar)):
             queue.dma_start(
-                out=out_1[0].rearrange("t (h j g) s -> h t j (g s)", h=HALVES, j=HALF)[h],
+                out=out_1[0].rearrange("t (j h g) s -> h t j (g s)", h=HALVES, j=HALF)[h],
                 in_=tw_rows[h * CHUNK : (h + 1) * CHUNK, :],
             )

@@ -27,6 +27,8 @@ CHUNK = FRAMES * HALF
 CHUNKS = 3
 ZEROS = 1
 SINGLE_FROM = 6
+GROUPED_FROM = 4
+MOVES = ((0, 1), (2, 3), (4,), (5,), (6,), (7,))
 PHI = 0
 THETA = 1
 FLOPS = 2 * (FRAMES * P) * FEATURES * (2 * LATENT) + 2 * FRAMES * P * P * LATENT + 2 * P * FRAMES * FRAMES * LATENT
@@ -94,6 +96,7 @@ def tile_higcin_volleyball_pa_kernel(tc, x, Wtheta, Wphi, out_0, out_1):
             words = plane[:].bitcast(I32)
             nc.vector.memset(words.rearrange("p (k c n) -> p k c n", k=GROUPS * 2, c=CHUNKS)[:, :, ZEROS, :], 0)
             g_views.append(words.rearrange(by_chunk, g=GROUPS, w=2, c=CHUNKS, t=FRAMES))
+        g_bytes_view = g_scales[:].rearrange(by_chunk, g=GROUPS, w=2, c=CHUNKS, t=FRAMES)
         masked = keep.tile([P, GROUPS * FRAMES, HALF], F32, name="masked")
         tw_rows = keep.tile([P, GROUPS * FRAMES], F32, name="tw_rows")
         warm_bank = first_bank.tile([P, BANK], F32, tag="first", name="warm_bank")
@@ -165,8 +168,11 @@ def tile_higcin_volleyball_pa_kernel(tc, x, Wtheta, Wphi, out_0, out_1):
                         )
                 if f not in h_grouped:
                     h_grouped[f] = stage.tile([P, 2, P, PACK], BF16, tag="h_grouped", name="h_grouped", align_bytes=64)
-                target = h_grouped[f][:, w, :, :].rearrange("p (a j) i -> p a j i", j=HALF)
-                source = bank[:].rearrange("p i (j a) -> p a j i", j=HALF)
+                target = h_grouped[f][:, w, :, :]
+                source = bank[:].rearrange("p i r -> p r i")
+                if w == PHI or f >= GROUPED_FROM:
+                    target = target.rearrange("p (a j) i -> p a j i", j=HALF)
+                    source = bank[:].rearrange("p i (j a) -> p a j i", j=HALF)
                 if (f, w) in VECTOR_LOWERS:
                     quantise_waiting(0)
                     nc.vector.tensor_copy(out=target, in_=source)
@@ -186,21 +192,38 @@ def tile_higcin_volleyball_pa_kernel(tc, x, Wtheta, Wphi, out_0, out_1):
                 in_=h_grouped[f][:, w_from:w_to, :, :].rearrange("p w r i -> p (w r i)"),
             )
             move_unmoved()
-            unmoved["piece"] = (f, w_from, w_to)
+            for frames in MOVES:
+                if f == frames[-1]:
+                    unmoved["piece"] = (frames[0], f + 1, w_from, w_to)
             if (f, w_from) == (FRAMES - 1, THETA):
                 move_unmoved()
 
         def move_unmoved():
             if "piece" not in unmoved:
                 return
-            f, w_from, w_to = unmoved.pop("piece")
-            for plain, nodes, by_group in ((h_codes, 1, g_views[0]), (h_scales, 4, g_views[1])):
-                nc.vector.tensor_copy(
-                    out=by_group[:, w_from:w_to, :, 0:CHUNKS:2, f, :].rearrange("p w g h j -> p w h g j"),
-                    in_=plain[:, f, :]
-                    .bitcast(I32)[:, w_from * P // nodes : w_to * P // nodes]
-                    .rearrange("p (w h g j) -> p w h g j", w=w_to - w_from, g=GROUPS, h=HALVES),
-                )
+            f_from, f_to, w_from, w_to = unmoved.pop("piece")
+            if f_from < GROUPED_FROM:
+                for plain, by_group in ((h_codes[:].bitcast(I32), g_views[0]), (h_scales[:], g_bytes_view)):
+                    nc.vector.tensor_copy(
+                        out=by_group[:, THETA, :, 0:CHUNKS:2, f_from:f_to, :],
+                        in_=plain[:, f_from:f_to, P : 2 * P].rearrange("p t (j h g) -> p g h t j", h=HALVES, g=GROUPS),
+                    )
+                for plain, nodes, by_group in ((h_codes, 1, g_views[0]), (h_scales, 4, g_views[1])):
+                    nc.vector.tensor_copy(
+                        out=by_group[:, PHI, :, 0:CHUNKS:2, f_from:f_to, :],
+                        in_=plain[:, f_from:f_to, :]
+                        .bitcast(I32)[:, :, 0 : P // nodes]
+                        .rearrange("p t (h g j) -> p g h t j", g=GROUPS, h=HALVES),
+                    )
+                return
+            for w in range(w_from, w_to):
+                for plain, nodes, by_group in ((h_codes, 1, g_views[0]), (h_scales, 4, g_views[1])):
+                    nc.vector.tensor_copy(
+                        out=by_group[:, w, :, 0:CHUNKS:2, f_from, :],
+                        in_=plain[:, f_from, :]
+                        .bitcast(I32)[:, w * P // nodes : (w + 1) * P // nodes]
+                        .rearrange("p (h g j) -> p g h j", g=GROUPS, h=HALVES),
+                    )
 
         def spatial(bank, f):
             nc.tensor.matmul_mx(
@@ -221,6 +244,9 @@ def tile_higcin_volleyball_pa_kernel(tc, x, Wtheta, Wphi, out_0, out_1):
                 in_=bank[:, used, :].rearrange("p f (a j) -> p f j a", j=HALF),
                 mul=1.0 / P,
             )
+            if f_to <= GROUPED_FROM:
+                nc.sync.dma_start(out=out_0[0, f_from:f_to].rearrange("t j k -> j t k"), in_=sw_rows[:, used, :])
+                return
             for f in range(f_from, f_to):
                 rows_by_group = out_0[0, f].rearrange("(j a) k -> a j k", j=HALF)
                 nc.sync.dma_start(out=rows_by_group, in_=sw_rows[:, f % 4, :])

@@ -245,11 +245,13 @@ def tile_higcin_volleyball_pa_kernel(tc, x, Wtheta, Wphi, out_0, out_1):
                 mul=1.0 / P,
             )
             if f_to <= GROUPED_FROM:
-                nc.sync.dma_start(out=out_0[0, f_from:f_to].rearrange("t j k -> j t k"), in_=sw_rows[:, used, :])
+                for queue, f in ((nc.sync, 0), (nc.scalar, 2)):
+                    queue.dma_start(out=out_0[0, f : f + 2].rearrange("t j k -> j t k"), in_=sw_rows[:, f : f + 2, :])
                 return
             for f in range(f_from, f_to):
                 rows_by_group = out_0[0, f].rearrange("(j a) k -> a j k", j=HALF)
-                nc.sync.dma_start(out=rows_by_group, in_=sw_rows[:, f % 4, :])
+                queue = (nc.sync, nc.scalar)[f % 2]
+                queue.dma_start(out=rows_by_group, in_=sw_rows[:, f % 4, :])
 
         def temporal(bank, g):
             first_phi = (2 * g + PHI) * CHUNKS * CHUNK

@@ -35,7 +35,7 @@ FLOPS = 2 * (FRAMES * P) * FEATURES * (2 * LATENT) + 2 * FRAMES * P * P * LATENT
 
 VECTOR_EMPTIES = (("x", 5), ("x", 6))
 VECTOR_LOWERS = ((1, THETA),)
-UNSORTED = (("theta", 0), ("theta", 1), ("x", 1), ("x", 2))
+UNSORTED = (("theta", 0), ("x", 1), ("x", 2))
 SORT_AHEAD = 3
 WARM_BEFORE = 5
 WARM_BEHIND = (("theta", 0), ("theta", 1), ("theta", 2), ("theta", 3), ("x", 1), ("x", 2))
@@ -236,17 +236,18 @@ def tile_higcin_volleyball_pa_kernel(tc, x, Wtheta, Wphi, out_0, out_1):
                 stop=True,
             )
 
-        def store_spatial(bank, f_from, f_to):
+        def store_spatial(bank, f_from, f_to, on_vector):
             sw_rows = stage.tile([P, 4, P], F32, tag="sw_rows", name="sw_rows")
             used = slice(f_from % 4, (f_to - 1) % 4 + 1)
-            nc.scalar.mul(
-                out=sw_rows[:, used, :].rearrange("p f (j a) -> p f j a", j=HALF),
-                in_=bank[:, used, :].rearrange("p f (a j) -> p f j a", j=HALF),
-                mul=1.0 / P,
-            )
+            target = sw_rows[:, used, :].rearrange("p f (j a) -> p f j a", j=HALF)
+            source = bank[:, used, :].rearrange("p f (a j) -> p f j a", j=HALF)
+            if on_vector:
+                nc.vector.tensor_scalar_mul(out=target, in0=source, scalar1=1.0 / P)
+            else:
+                nc.scalar.mul(out=target, in_=source, mul=1.0 / P)
             if f_to <= GROUPED_FROM:
-                for queue, f in ((nc.sync, 0), (nc.scalar, 2)):
-                    queue.dma_start(out=out_0[0, f : f + 2].rearrange("t j k -> j t k"), in_=sw_rows[:, f : f + 2, :])
+                queue = (nc.sync, nc.scalar)[f_from // 2]
+                queue.dma_start(out=out_0[0, f_from:f_to].rearrange("t j k -> j t k"), in_=sw_rows[:, used, :])
                 return
             for f in range(f_from, f_to):
                 rows_by_group = out_0[0, f].rearrange("(j a) k -> a j k", j=HALF)
@@ -301,14 +302,15 @@ def tile_higcin_volleyball_pa_kernel(tc, x, Wtheta, Wphi, out_0, out_1):
         sw_last = banks.tile([P, 4, P], F32, tag="bank", name="sw_last")
         for f in range(4):
             spatial(sw_early, f)
-        store_spatial(sw_early, 0, 4)
+        store_spatial(sw_early, 0, 2, False)
+        store_spatial(sw_early, 2, 4, False)
         for f in range(4, FRAMES - 1):
             spatial(sw_late, f)
-        store_spatial(sw_late, 4, FRAMES - 1)
+        store_spatial(sw_late, 4, FRAMES - 1, True)
         for i in range(WARM_LAST):
             warm_up(banks.tile([P, BANK], F32, tag="bank", name="idle_bank"))
         spatial(sw_last, FRAMES - 1)
-        store_spatial(sw_last, FRAMES - 1, FRAMES)
+        store_spatial(sw_last, FRAMES - 1, FRAMES, False)
         tw_banks = [banks.tile([P, 2, P], F32, tag="bank", name="tw_bank") for pair in range(3)]
         tw_banks.append(banks.tile([P, 2, P], F32, tag="bank", name="tw_bank"))
         for g in range(GROUPS):

from contextlib import ExitStack

import concourse.mybir as mybir
from concourse.masks import make_identity

F32 = mybir.dt.float32
BF16 = mybir.dt.bfloat16
U32 = mybir.dt.uint32
I32 = mybir.dt.int32
U8 = mybir.dt.uint8
FP8X4 = mybir.dt.float8_e4m3fn_x4
ALU = mybir.AluOpType
AX = mybir.AxisListType

P = 128
FRAMES = 8
FEATURES = 1024
LATENT = 512
PACK = 4
PASSES = FEATURES // (P * PACK)
BANK = 512
GROUP = 16
GROUPS = P // GROUP
HALVES = 2
HALF = GROUP // HALVES
CHUNK = FRAMES * HALF
CHUNKS = 3
ZEROS = 1
SINGLE_FROM = 6
GROUPED_FROM = 4
MOVES = ((0, 1), (2, 3), (4,), (5,), (6,), (7,))
PHI = 0
THETA = 1
FLOPS = 2 * (FRAMES * P) * FEATURES * (2 * LATENT) + 2 * FRAMES * P * P * LATENT + 2 * P * FRAMES * FRAMES * LATENT

VECTOR_EMPTIES = (("x", 5), ("x", 6))
VECTOR_LOWERS = ((1, THETA),)
UNSORTED = (("theta", 0), ("x", 1), ("x", 2))
SORT_AHEAD = 3
WARM_BEFORE = 5
WARM_BEHIND = (("theta", 0), ("theta", 1), ("theta", 2), ("theta", 3), ("x", 1), ("x", 2))
WARM_LAST = 2


def tile_higcin_volleyball_pa_kernel(tc, x, Wtheta, Wphi, out_0, out_1):
    nc = tc.nc
    with ExitStack() as ctx:
        ctx.enter_context(tc.manual_schedule())
        raw = ctx.enter_context(tc.tile_pool(name="raw", bufs=1))
        keep = ctx.enter_context(tc.tile_pool(name="keep", bufs=1))
        stage = ctx.enter_context(tc.tile_pool(name="stage", bufs=6))
        banks = ctx.enter_context(tc.psum_pool(name="banks", bufs=7))
        first_bank = ctx.enter_context(tc.psum_pool(name="first", bufs=1))

        theta_tiles = [("theta", i) for i in range(PACK)]
        phi_tiles = [("phi", i) for i in range(PACK)]
        x_tiles = [("x", f) for f in range(FRAMES)]
        tiles = theta_tiles + x_tiles[0:3] + phi_tiles + x_tiles[3:8]

        dram = {}
        for i in range(PACK):
            dram[("theta", i)] = Wtheta.rearrange("(p i) d -> p i d", i=PACK)[:, i, :]
            dram[("phi", i)] = Wphi.rearrange("(p i) d -> p i d", i=PACK)[:, i, :]
        for f in range(FRAMES):
            dram[("x", f)] = x[0, f]
        rows = {}
        codes = {}
        scales = {}
        for key in tiles:
            label = "%s%d" % key
            rows[key] = raw.tile([P, FEATURES], BF16, name="rows_" + label)
            codes[key] = keep.tile([P, PASSES * P], U32, name="codes_" + label, align_bytes=64)
            scales[key] = keep.tile([P, PASSES * P], U8, name="scales_" + label, align_bytes=64)
            nc.sync.dma_start(out=rows[key][:], in_=dram[key])

        zeros = keep.tile([P, BANK], BF16, name="zeros")
        nc.vector.memset(zeros[:], 0.0)
        table_load = keep.tile([P, 1], F32, name="table_load")
        nc.scalar.mul(out=table_load[:], in_=zeros[:, 0:1], mul=1.0)
        ident = keep.tile([P, P], F32, name="ident")
        make_identity(nc, ident[:])
        h_codes = keep.tile([P, FRAMES, 2 * P], U32, name="h_codes", align_bytes=64)
        h_scales = keep.tile([P, FRAMES, 2 * P], U8, name="h_scales", align_bytes=64)
        nc.vector.memset(h_scales[:].rearrange("p f n -> p (f n)").bitcast(I32), 0)
        block_sum = keep.tile([P, HALF], F32, name="block_sum")
        nc.vector.tensor_reduce(
            out=block_sum[:], in_=ident[:].rearrange("p (b j) -> p j b", j=HALF), axis=AX.X, op=ALU.add
        )
        same_node = keep.tile([P, HALF], F32, name="same_node")
        nc.vector.tensor_scalar_mul(out=same_node[:], in0=block_sum[:], scalar1=1.0 / FRAMES)
        g_codes = keep.tile([P, GROUPS * 2 * CHUNKS * CHUNK], U32, name="g_codes", align_bytes=64)
        g_scales = keep.tile([P, GROUPS * 2 * CHUNKS * CHUNK], U8, name="g_scales", align_bytes=64)
        by_chunk = "p (g w c t j) -> p w g c t j"
        g_views = []
        for plane in (g_codes, g_scales):
            words = plane[:].bitcast(I32)
            nc.vector.memset(words.rearrange("p (k c n) -> p k c n", k=GROUPS * 2, c=CHUNKS)[:, :, ZEROS, :], 0)
            g_views.append(words.rearrange(by_chunk, g=GROUPS, w=2, c=CHUNKS, t=FRAMES))
        g_bytes_view = g_scales[:].rearrange(by_chunk, g=GROUPS, w=2, c=CHUNKS, t=FRAMES)
        masked = keep.tile([P, GROUPS * FRAMES, HALF], F32, name="masked")
        tw_rows = keep.tile([P, GROUPS * FRAMES], F32, name="tw_rows")
        warm_bank = first_bank.tile([P, BANK], F32, tag="first", name="warm_bank")

        def warm_up(bank):
            nc.tensor.matmul(out=bank[:], lhsT=zeros[:, 0:P], rhs=zeros[:], start=True, stop=True)

        ordered = {}
        waiting = []

        def quantise_waiting(keep_back):
            while len(waiting) > keep_back:
                step = waiting.pop(0)
                step[0](*step[1:])

        def sort_words(key):
            ordered[key] = stage.tile([P, PASSES, 2, P], F32, tag="ordered", name="ordered")
            nc.vector.tensor_copy(
                out=ordered[key][:], in_=rows[key][:].bitcast(F32).rearrange("p (c r h) -> p c h r", c=PASSES, h=2)
            )

        def transpose_run(keys):
            for key in keys:
                place = tiles.index(key)
                for ahead in tiles[place : place + SORT_AHEAD + 1]:
                    if ahead not in ordered and ahead not in UNSORTED:
                        sort_words(ahead)
                bank = banks.tile([P, PASSES, 2, P], F32, tag="bank", name="bank")
                words = rows[key][:].bitcast(F32).rearrange("p (c r h) -> p c h r", c=PASSES, h=2)
                if key in ordered:
                    words = ordered[key][:]
                for c in range(PASSES):
                    for h in range(2):
                        nc.tensor.transpose(bank[:, c, h, :], words[:, c, h, :], ident[:])
                if key in WARM_BEHIND:
                    warm_up(warm_bank)
                grouped = stage.tile([P, FEATURES], BF16, tag="grouped", name="grouped", align_bytes=64)
                target = grouped[:].bitcast(F32).rearrange("p (c r h) -> p c r h", c=PASSES, h=2)
                source = bank[:].rearrange("p c h r -> p c r h")
                if key in VECTOR_EMPTIES:
                    quantise_waiting(0)
                    nc.vector.tensor_copy(out=target, in_=source)
                else:
                    nc.scalar.copy(out=target, in_=source)
                waiting.append((quantise_tile, key, grouped))
                quantise_waiting(1)

        def quantise_tile(key, grouped):
            nc.vector.quantize_mx(out=codes[key][:].bitcast(FP8X4), scales=scales[key][:], in_=grouped[:])

        h_grouped = {}
        unmoved = {}

        def project_run(pairs):
            for f, w in pairs:
                bank = banks.tile([P, PACK, P], F32, tag="bank", name="bank")
                for i in range(PACK):
                    weight = (("phi", i), ("theta", i))[w]
                    for c in range(PASSES):
                        cols = slice(c * P, (c + 1) * P)
                        nc.tensor.matmul_mx(
                            out=bank[:, i, :],
                            lhsT=codes[weight][:, cols].bitcast(FP8X4),
                            lhsT_scale=scales[weight][:, cols],
                            rhs=codes[("x", f)][:, cols].bitcast(FP8X4),
                            rhs_scale=scales[("x", f)][:, cols],
                            start=(c == 0),
                            stop=(c == PASSES - 1),
                        )
                if f not in h_grouped:
                    h_grouped[f] = stage.tile([P, 2, P, PACK], BF16, tag="h_grouped", name="h_grouped", align_bytes=64)
                target = h_grouped[f][:, w, :, :]
                source = bank[:].rearrange("p i r -> p r i")
                if w == PHI or f >= GROUPED_FROM:
                    target = target.rearrange("p (a j) i -> p a j i", j=HALF)
                    source = bank[:].rearrange("p i (j a) -> p a j i", j=HALF)
                if (f, w) in VECTOR_LOWERS:
                    quantise_waiting(0)
                    nc.vector.tensor_copy(out=target, in_=source)
                else:
                    nc.scalar.copy(out=target, in_=source)
                if f >= SINGLE_FROM:
                    waiting.append((quantise_h, f, w, w + 1))
                elif w == PHI:
                    waiting.append((quantise_h, f, PHI, THETA + 1))
                quantise_waiting(1)

        def quantise_h(f, w_from, w_to):
            cols = slice(w_from * P, w_to * P)
            nc.vector.quantize_mx(
                out=h_codes[:, f, cols].bitcast(FP8X4),
                scales=h_scales[:, f, cols],
                in_=h_grouped[f][:, w_from:w_to, :, :].rearrange("p w r i -> p (w r i)"),
            )
            move_unmoved()
            for frames in MOVES:
                if f == frames[-1]:
                    unmoved["piece"] = (frames[0], f + 1, w_from, w_to)
            if (f, w_from) == (FRAMES - 1, THETA):
                move_unmoved()

        def move_unmoved():
            if "piece" not in unmoved:
                return
            f_from, f_to, w_from, w_to = unmoved.pop("piece")
            if f_from < GROUPED_FROM:
                for plain, by_group in ((h_codes[:].bitcast(I32), g_views[0]), (h_scales[:], g_bytes_view)):
                    nc.vector.tensor_copy(
                        out=by_group[:, THETA, :, 0:CHUNKS:2, f_from:f_to, :],
                        in_=plain[:, f_from:f_to, P : 2 * P].rearrange("p t (j h g) -> p g h t j", h=HALVES, g=GROUPS),
                    )
                for plain, nodes, by_group in ((h_codes, 1, g_views[0]), (h_scales, 4, g_views[1])):
                    nc.vector.tensor_copy(
                        out=by_group[:, PHI, :, 0:CHUNKS:2, f_from:f_to, :],
                        in_=plain[:, f_from:f_to, :]
                        .bitcast(I32)[:, :, 0 : P // nodes]
                        .rearrange("p t (h g j) -> p g h t j", g=GROUPS, h=HALVES),
                    )
                return
            for w in range(w_from, w_to):
                for plain, nodes, by_group in ((h_codes, 1, g_views[0]), (h_scales, 4, g_views[1])):
                    nc.vector.tensor_copy(
                        out=by_group[:, w, :, 0:CHUNKS:2, f_from, :],
                        in_=plain[:, f_from, :]
                        .bitcast(I32)[:, w * P // nodes : (w + 1) * P // nodes]
                        .rearrange("p (h g j) -> p g h j", g=GROUPS, h=HALVES),
                    )

        def spatial(bank, f):
            nc.tensor.matmul_mx(
                out=bank[:, f % 4, :],
                lhsT=h_codes[:, f, P : 2 * P].bitcast(FP8X4),
                lhsT_scale=h_scales[:, f, P : 2 * P],
                rhs=h_codes[:, f, 0:P].bitcast(FP8X4),
                rhs_scale=h_scales[:, f, 0:P],
                start=True,
                stop=True,
            )

        def store_spatial(bank, f_from, f_to, on_vector):
            sw_rows = stage.tile([P, 4, P], F32, tag="sw_rows", name="sw_rows")
            used = slice(f_from % 4, (f_to - 1) % 4 + 1)
            target = sw_rows[:, used, :].rearrange("p f (j a) -> p f j a", j=HALF)
            source = bank[:, used, :].rearrange("p f (a j) -> p f j a", j=HALF)
            if on_vector:
                nc.vector.tensor_scalar_mul(out=target, in0=source, scalar1=1.0 / P)
            else:
                nc.scalar.mul(out=target, in_=source, mul=1.0 / P)
            if f_to <= GROUPED_FROM:
                queue = (nc.sync, nc.scalar)[f_from // 2]
                queue.dma_start(out=out_0[0, f_from:f_to].rearrange("t j k -> j t k"), in_=sw_rows[:, used, :])
                return
            for f in range(f_from, f_to):
                rows_by_group = out_0[0, f].rearrange("(j a) k -> a j k", j=HALF)
                queue = (nc.sync, nc.scalar)[f % 2]
                queue.dma_start(out=rows_by_group, in_=sw_rows[:, f % 4, :])

        def temporal(bank, g):
            first_phi = (2 * g + PHI) * CHUNKS * CHUNK
            first_theta = (2 * g + THETA) * CHUNKS * CHUNK
            for h in range(HALVES):
                still = slice(first_theta + h * CHUNK, first_theta + h * CHUNK + P)
                moving = slice(first_phi + 2 * h * CHUNK, first_phi + 2 * h * CHUNK + P)
                nc.tensor.matmul_mx(
                    out=bank[:, g % 2, :],
                    lhsT=g_codes[:, still].bitcast(FP8X4),
                    lhsT_scale=g_scales[:, still],
                    rhs=g_codes[:, moving].bitcast(FP8X4),
                    rhs_scale=g_scales[:, moving],
                    start=(h == 0),
                    stop=(h == HALVES - 1),
                )

        def keep_same_node(bank, g_from, g_to):
            count = g_to - g_from
            nc.vector.tensor_tensor(
                out=masked[:, g_from * FRAMES : g_to * FRAMES, :].rearrange("p (g s) j -> p g s j", s=FRAMES),
                in0=bank[:, :, 0:CHUNK].rearrange("p g (s j) -> p g s j", j=HALF),
                in1=same_node[:].unsqueeze(1).unsqueeze(1).to_broadcast([P, count, FRAMES, HALF]),
                op=ALU.mult,
            )

        def sum_nodes(g_from, g_to):
            pairs = slice(g_from * FRAMES, g_to * FRAMES)
            nc.vector.tensor_reduce(out=tw_rows[:, pairs], in_=masked[:, pairs, :], axis=AX.X, op=ALU.add)

        for i in range(WARM_BEFORE):
            warm_up(warm_bank)
        transpose_run(theta_tiles + x_tiles[0:3] + phi_tiles[0:2])
        project_run([(0, THETA)])
        transpose_run(phi_tiles[2:4] + x_tiles[3:4])
        project_run([(1, THETA), (2, THETA)])
        transpose_run(x_tiles[4:6])
        project_run([(0, PHI), (1, PHI), (3, THETA)])
        transpose_run(x_tiles[6:8])
        project_run([(2, PHI), (3, PHI)])
        project_run([(f, w) for f in range(4, FRAMES) for w in (THETA, PHI)])
        quantise_waiting(0)
        move_unmoved()

        sw_early = first_bank.tile([P, 4, P], F32, tag="first", name="sw_early")
        sw_late = banks.tile([P, 4, P], F32, tag="bank", name="sw_late")
        sw_last = banks.tile([P, 4, P], F32, tag="bank", name="sw_last")
        for f in range(4):
            spatial(sw_early, f)
        store_spatial(sw_early, 0, 2, False)
        store_spatial(sw_early, 2, 4, False)
        for f in range(4, FRAMES - 1):
            spatial(sw_late, f)
        store_spatial(sw_late, 4, FRAMES - 1, True)
        for i in range(WARM_LAST):
            warm_up(banks.tile([P, BANK], F32, tag="bank", name="idle_bank"))
        spatial(sw_last, FRAMES - 1)
        store_spatial(sw_last, FRAMES - 1, FRAMES, False)
        tw_banks = [banks.tile([P, 2, P], F32, tag="bank", name="tw_bank") for pair in range(3)]
        tw_banks.append(banks.tile([P, 2, P], F32, tag="bank", name="tw_bank"))
        for g in range(GROUPS):
            temporal(tw_banks[g // 2], g)
        for pair in range(5):
            if pair < 4:
                keep_same_node(tw_banks[pair], 2 * pair, 2 * pair + 2)
            if pair > 0:
                sum_nodes(2 * pair - 2, 2 * pair)
        for h, queue in enumerate((nc.sync, nc.scalar)):
            queue.dma_start(
                out=out_1[0].rearrange("t (j h g) s -> h t j (g s)", h=HALVES, j=HALF)[h],
                in_=tw_rows[h * CHUNK : (h + 1) * CHUNK, :],
            )
